import numpy as np
import ml_dtypes


def mxq(x, axis, fmt="e4m3"):
    dtype, down = {"e4m3": (ml_dtypes.float8_e4m3fn, 7), "e5m2": (ml_dtypes.float8_e5m2, 14)}[fmt]
    v = np.moveaxis(np.asarray(x, np.float32).astype(ml_dtypes.bfloat16).astype(np.float64), axis, -1)
    blocks = v.reshape(v.shape[:-1] + (-1, 32))
    amax = np.abs(blocks).max(-1, keepdims=True)
    byte = np.maximum(np.where(amax > 0, np.frexp(amax)[1] - 1 + 127, 0) - down, 1)
    scale = np.exp2(byte - 127.0)
    codes = (blocks / scale).astype(np.float32).astype(dtype).astype(np.float64)
    return np.moveaxis((codes * scale).reshape(v.shape), -1, axis)


WIDE = False


def mx_kscale(k):
    if not WIDE:
        return np.ones(k)
    levels = np.array([10, -10, 5, -5, 0])
    if k % 512:
        return np.exp2(np.random.permutation(np.resize(levels, k // 32))).repeat(32)
    a = np.empty((k // 512, 16))
    for p in range(k // 512):
        a[p, :8] = np.random.permutation(np.resize(levels, 8))
        for g in range(8):
            far = levels[np.abs(levels - a[p, g]) >= 10]
            a[p, g + 8] = far[np.random.randint(len(far))]
    return np.exp2(a.ravel()).repeat(32)


BF16 = ml_dtypes.bfloat16


def bf(x):
    return np.asarray(x, np.float32).astype(BF16)


def f64(x):
    return np.asarray(x).astype(np.float64)


B, H = 4096, 512
K = 2 * H
BETA_SHIFT = 1.0
LN_EPS = 1e-5
BAG_EPS = 1e-6


def setup_inputs():
    s = mx_kscale(H)
    r_main = np.random.uniform(0.5, 1.1, (B, 1))
    r_branch = np.random.uniform(0.5, 1.1, (B, 1))
    w_mb = np.random.standard_normal((K, H)) / np.sqrt(K)
    w_mb[H:] = w_mb[H:] / s[:, None]
    return {"main": bf(np.random.standard_normal((B, H)) * r_main),
            "branch": bf(np.random.standard_normal((B, H)) * r_branch * s),
            "o": bf(1.0 - np.random.random((B, 1)) * np.random.uniform(0.2, 0.8, (B, H))),
            "is_bag": bf(np.random.random((B, 1))),
            "W_mb": bf(w_mb),
            "b_mb": bf(np.random.standard_normal(H) * 0.3),
            "W_b": bf(np.random.standard_normal((H, H)) * 2.0 / np.sqrt(H) / s[:, None]),
            "b_b": bf(np.random.standard_normal(H) * 0.3),
            "ln_g": bf(1.0 + 0.1 * np.random.standard_normal(H)),
            "ln_b": bf(0.1 * np.random.standard_normal(H))}


def reference(main, branch, o, is_bag, W_mb, b_mb, W_b, b_b, ln_g, ln_b):
    main, is_bag = f64(main), f64(is_bag)
    mbq = mxq(np.concatenate([main, f64(branch)], axis=-1), 1, "e4m3")
    weight_b = np.maximum((mbq @ mxq(f64(W_mb), 0, "e4m3")) + f64(b_mb), 0.0)
    h_m = weight_b * ((mbq[:, H:] @ mxq(f64(W_b), 0, "e4m3")) + f64(b_b))
    em_norm = np.sqrt((main ** 2).sum(-1))
    hm_norm = np.sqrt((h_m ** 2).sum(-1))
    hm_norm = np.where(hm_norm == 0, np.ones_like(hm_norm), hm_norm)
    alpha = np.minimum(em_norm / (hm_norm + BAG_EPS) * BETA_SHIFT, 1.0)[:, None]
    pre = alpha * h_m + main
    mu = pre.mean(-1, keepdims=True)
    var = ((pre - mu) ** 2).mean(-1, keepdims=True)
    emb = (pre - mu) / np.sqrt(var + LN_EPS) * f64(ln_g) + f64(ln_b)
    shift_c = emb * is_bag + main * (1.0 - is_bag)
    h = f64(o) * np.tanh(shift_c)
    return h, shift_c

@@ -1,0 +1,411 @@
+from contextlib import ExitStack
+
+import concourse.masks as masks
+import concourse.mybir as mybir
+
+F32 = mybir.dt.float32
+BF16 = mybir.dt.bfloat16
+U8 = mybir.dt.uint8
+U32 = mybir.dt.uint32
+I32 = mybir.dt.int32
+FP8X4 = mybir.dt.float8_e4m3fn_x4
+ALU = mybir.AluOpType
+ACT = mybir.ActivationFunctionType
+
+P = 128
+ROWS = 4096
+H = 512
+TILES = ROWS // P
+TG = 4
+GROUPS = TILES // TG
+GROUP_ROWS = TG * P
+CHUNKS = H // P
+LN_EPS = 1e-5
+BAG_EPS = 1e-6
+
+FLOPS = 2 * ROWS * (2 * H + H) * H
+
+LAG_QUANTISE = -2
+LAG_NORM = 1
+LAG_PRE = 2
+LAG_STATS = 3
+LAG_CARRY = 3
+LAG_OUT = 4
+LOAD_AHEAD = 1
+
+
+def tile_bag_lstm_pb_t_kernel(
+    tc, main, branch, o, is_bag, W_mb, b_mb, W_b, b_b, ln_g, ln_b, out_0, out_1
+):
+    nc = tc.nc
+    main_v = main.rearrange("(p j) col -> p j col", j=TILES)
+    branch_v = branch.rearrange("(p j) col -> p j col", j=TILES)
+    o_v = o.rearrange("(p j) col -> p j col", j=TILES)
+    h_v = out_0.rearrange("(p j) col -> p j col", j=TILES)
+    shift_v = out_1.rearrange("(p j) col -> p j col", j=TILES)
+
+    with ExitStack() as ctx:
+        const = ctx.enter_context(tc.tile_pool(name="const", bufs=1))
+        inputs = ctx.enter_context(tc.tile_pool(name="inputs", bufs=3))
+        work = ctx.enter_context(tc.tile_pool(name="work", bufs=3))
+        small = ctx.enter_context(tc.tile_pool(name="small", bufs=3))
+        psum_g = ctx.enter_context(tc.psum_pool(name="psum_g", bufs=1))
+        psum = ctx.enter_context(tc.psum_pool(name="psum", bufs=7))
+        ctx.enter_context(tc.manual_schedule())
+
+        live = {}
+
+        def bank(shape, dtype=F32):
+            return psum.tile(shape, dtype, name="bank", tag="bank")
+
+        def per_row(name, g, width=TG):
+            if (name, g) not in live:
+                live[(name, g)] = small.tile([P, width], F32, name=name, tag=name)
+            return live[(name, g)]
+
+        def unread():
+            return work.tile([P, H], BF16, name="unread", tag="unread", bufs=4)
+
+        def tiles_of(g):
+            return slice(g * TG, (g + 1) * TG)
+
+        def two_tiles_of(g, half):
+            return slice(g * TG + 2 * half, g * TG + 2 * half + 2)
+
+        def exists(g):
+            return 0 <= g < GROUPS
+
+        def load_weights(s):
+            if s < 2:
+                rows = W_mb.rearrange("(s p v) n -> s p v n", s=2, p=P, v=4)[s]
+            else:
+                rows = W_b.rearrange("(p v) n -> p v n", p=P, v=4)
+            nc.sync.dma_start(out=w_rows[:, s], in_=rows)
+
+        def load_states(g):
+            if not exists(g):
+                return
+            live[("main", g)] = inputs.tile([P, TG, H], BF16, name="main_t", tag="main", bufs=7)
+            nc.sync.dma_start(out=live[("main", g)][:], in_=main_v[:, tiles_of(g), :])
+            live[("branch", g)] = inputs.tile([P, TG, H], BF16, name="branch_t", tag="branch")
+            nc.sync.dma_start(out=live[("branch", g)][:], in_=branch_v[:, tiles_of(g), :])
+
+        def load_o(g):
+            if not exists(g):
+                return
+            live[("o", g)] = inputs.tile([P, TG, H], BF16, name="o_t", tag="o")
+            nc.sync.dma_start(out=live[("o", g)][:], in_=o_v[:, tiles_of(g), :])
+
+        w_rows = const.tile([P, 3, 4, H], BF16, name="w_rows")
+        w_grouped = const.tile([P, 3, H, 4], BF16, name="w_grouped", align_bytes=64)
+        w_words = const.tile([P, 3, H], U32, name="w_words", align_bytes=64)
+        w_scales = const.tile([P, 3, H], U8, name="w_scales", align_bytes=64)
+        table_warm = const.tile([P, 1], F32, name="table_warm")
+        ident_f = const.tile([P, P], F32, name="ident_f")
+        ident_b = const.tile([P, P], BF16, name="ident_b")
+        ones_b = const.tile([P, P], BF16, name="ones_b")
+        exp_half = const.tile([P, 2 * TG], F32, name="exp_half")
+        exp_minus_half = const.tile([P, TG], F32, name="exp_minus_half")
+        exp_minus_one = const.tile([P, TG], F32, name="exp_minus_one")
+        bias_rows = const.tile([P, P], BF16, name="bias_rows")
+        ln_rows = const.tile([P, 2 * H], BF16, name="ln_rows")
+        bag_b = const.tile([P, TILES], BF16, name="bag_b")
+        bag = const.tile([P, TILES], F32, name="bag")
+        not_bag = const.tile([P, TILES], F32, name="not_bag")
+        bias_cols = const.tile([P, 2 * CHUNKS], F32, name="bias_cols")
+        ln_b_all = const.tile([P, H], BF16, name="ln_b_all")
+        bag_diag = const.tile([P, TILES, P], BF16, name="bag_diag")
+        ln_g_all = psum_g.tile([P, H], F32, name="ln_g_all")
+
+        for s in range(3):
+            load_weights(s)
+        for g in range(LOAD_AHEAD):
+            load_states(g)
+
+        nc.vector.memset(table_warm[:], 0.0)
+        nc.scalar.dma_start(out=bag_b[:], in_=is_bag.rearrange("(p j) one -> p (j one)", j=TILES))
+        nc.vector.memset(bias_rows[:].bitcast(I32), 0)
+        nc.scalar.dma_start(out=bias_rows[0:CHUNKS, :], in_=b_mb.rearrange("(a x) -> a x", x=P))
+        nc.scalar.dma_start(out=bias_rows[CHUNKS : 2 * CHUNKS, :], in_=b_b.rearrange("(a x) -> a x", x=P))
+        nc.vector.memset(ln_rows[:].bitcast(I32), 0)
+        nc.scalar.dma_start(out=ln_rows[0:1, 0:H], in_=ln_g.unsqueeze(0))
+        nc.scalar.dma_start(out=ln_rows[0:1, H : 2 * H], in_=ln_b.unsqueeze(0))
+        nc.scalar.activation(out=table_warm[:], in_=table_warm[:], func=ACT.Tanh)
+        masks.make_identity(nc, ident_f[:])
+        masks.make_identity(nc, ident_b[:])
+        nc.vector.memset(ones_b[:], 1.0)
+        nc.vector.memset(exp_half[:], 0.5)
+        nc.vector.memset(exp_minus_half[:], -0.5)
+        nc.vector.memset(exp_minus_one[:], -1.0)
+        nc.vector.tensor_copy(out=bag[:], in_=bag_b[:])
+        nc.vector.tensor_scalar(
+            out=not_bag[:], in0=bag_b[:], scalar1=-1.0, scalar2=1.0, op0=ALU.mult, op1=ALU.add
+        )
+        bias_t = bank([P, P], BF16)
+        nc.tensor.transpose(bias_t[:], bias_rows[:], ident_b[:])
+        nc.vector.tensor_copy(out=bias_cols[:], in_=bias_t[:, 0 : 2 * CHUNKS])
+        nc.tensor.matmul(out=ln_g_all[:], lhsT=ones_b[:], rhs=ln_rows[:, 0:H], start=True, stop=True)
+        ln_b_bank = bank([P, H])
+        nc.tensor.matmul(out=ln_b_bank[:], lhsT=ones_b[:], rhs=ln_rows[:, H : 2 * H], start=True, stop=True)
+        nc.vector.tensor_copy(out=ln_b_all[:], in_=ln_b_bank[:])
+        for first in range(0, TILES, 8):
+            some = slice(first, first + 8)
+            nc.gpsimd.tensor_tensor(
+                out=bag_diag[:, some, :], in0=ident_b[:].unsqueeze(1).to_broadcast([P, 8, P]),
+                in1=bag_b[:, some].unsqueeze(2).to_broadcast([P, 8, P]), op=ALU.mult,
+            )
+
+        def group_weights(s, engine):
+            dst = w_grouped[:, s].rearrange("p (a i) v -> p a v i", i=4)
+            src = w_rows[:, s].rearrange("p v (a i) -> p a v i", i=4)
+            if engine == "scalar":
+                nc.scalar.copy(out=dst, in_=src)
+            else:
+                nc.vector.tensor_copy(out=dst, in_=src)
+
+        def quantise_weights(s):
+            nc.vector.quantize_mx(
+                out=w_words[:, s, :].bitcast(FP8X4),
+                scales=w_scales[:, s, :],
+                in_=w_grouped[:, s].rearrange("p n v -> p (n v)"),
+            )
+
+        group_weights(0, "vector")
+        group_weights(1, "scalar")
+        group_weights(2, "vector")
+        for s in range(3):
+            quantise_weights(s)
+
+        def k_to_partitions(g, i):
+            if not exists(g):
+                return
+            which = "main" if i < 2 else "branch"
+            half = i % 2
+            pairs = live[(which, g)][:].bitcast(F32)
+            turned = bank([P, 2, 2 * P])
+            for t in range(2):
+                for u in range(2):
+                    nc.tensor.transpose(
+                        turned[:, u, t * P : (t + 1) * P],
+                        pairs[:, 2 * half + t, u : 2 * P : 2],
+                        ident_f[:],
+                    )
+            if half == 0:
+                live[(which + "_k", g)] = work.tile(
+                    [P, 4 * GROUP_ROWS], BF16, name=which + "_k", tag=which + "_k", bufs=2, align_bytes=64
+                )
+            grouped = live[(which + "_k", g)][:].bitcast(F32).rearrange("p (row u) -> p row u", u=2)
+            nc.scalar.copy(
+                out=grouped[:, half * 2 * P : (half + 1) * 2 * P, :],
+                in_=turned[:].rearrange("p u row -> p row u"),
+            )
+
+        def quantise(g, which):
+            if not exists(g):
+                return
+            words_q = work.tile([P, GROUP_ROWS], U32, name=which + "_w", tag=which + "_w", align_bytes=64)
+            scales_q = work.tile([P, GROUP_ROWS], U8, name=which + "_s", tag=which + "_s", align_bytes=64)
+            nc.vector.quantize_mx(
+                out=words_q[:].bitcast(FP8X4), scales=scales_q[:], in_=live[(which + "_k", g)][:]
+            )
+            live[(which + "_q", g)] = (words_q, scales_q)
+
+        def gate_sums(g, c):
+            if not exists(g):
+                return
+            main_w, main_s = live[("main_q", g)]
+            branch_w, branch_s = live[("branch_q", g)]
+            cols = slice(c * P, (c + 1) * P)
+            sum_mb = bank([P, GROUP_ROWS])
+            nc.tensor.matmul_mx(
+                out=sum_mb[:], lhsT=w_words[:, 0, cols].bitcast(FP8X4), lhsT_scale=w_scales[:, 0, cols],
+                rhs=main_w[:].bitcast(FP8X4), rhs_scale=main_s[:], start=True, stop=False,
+            )
+            nc.tensor.matmul_mx(
+                out=sum_mb[:], lhsT=w_words[:, 1, cols].bitcast(FP8X4), lhsT_scale=w_scales[:, 1, cols],
+                rhs=branch_w[:].bitcast(FP8X4), rhs_scale=branch_s[:], start=False, stop=True,
+            )
+            sum_b = bank([P, GROUP_ROWS])
+            nc.tensor.matmul_mx(
+                out=sum_b[:], lhsT=w_words[:, 2, cols].bitcast(FP8X4), lhsT_scale=w_scales[:, 2, cols],
+                rhs=branch_w[:].bitcast(FP8X4), rhs_scale=branch_s[:], start=True, stop=True,
+            )
+            live[("sum_mb", g, c)] = sum_mb
+            live[("sum_b", g, c)] = sum_b
+
+        def gate_relu(g, c):
+            if not exists(g):
+                return
+            weight_b = work.tile([P, GROUP_ROWS], F32, name="weight_b", tag="weight_b")
+            live[("weight_b", g, c)] = weight_b
+            nc.scalar.activation(
+                out=weight_b[:], in_=live[("sum_mb", g, c)][:], func=ACT.Relu,
+                bias=bias_cols[:, c : c + 1], scale=1.0,
+            )
+
+        def gate_product(g, c):
+            if not exists(g) or c < 0:
+                return
+            if c == 0:
+                live[("h_m_t", g)] = work.tile([P, CHUNKS, GROUP_ROWS], F32, name="h_m_t", tag="h_m_t")
+            nc.vector.scalar_tensor_tensor(
+                out=live[("h_m_t", g)][:, c, :], in0=live[("sum_b", g, c)][:],
+                scalar=bias_cols[:, CHUNKS + c : CHUNKS + c + 1], in1=live[("weight_b", g, c)][:],
+                op0=ALU.add, op1=ALU.mult,
+            )
+
+        def rows_back(g, t):
+            h_m = bank([P, H])
+            for c in range(CHUNKS):
+                nc.tensor.transpose(
+                    h_m[:, c * P : (c + 1) * P], live[("h_m_t", g)][:, c, t * P : (t + 1) * P], ident_f[:]
+                )
+            return h_m
+
+        def norms(g, t):
+            if not exists(g):
+                return
+            squares = per_row("squares", g, 2 * TG)
+            h_m = rows_back(g, t)
+            nc.scalar.activation(
+                out=unread()[:], in_=live[("main", g)][:, t, :], func=ACT.Square,
+                accum_out=squares[:, t : t + 1],
+            )
+            nc.scalar.activation(
+                out=unread()[:], in_=h_m[:], func=ACT.Square, accum_out=squares[:, TG + t : TG + t + 1]
+            )
+
+        def alpha(g):
+            if not exists(g):
+                return
+            lengths = per_row("lengths", g, 2 * TG)
+            nc.gpsimd.tensor_tensor(
+                out=lengths[:], in0=per_row("squares", g, 2 * TG)[:], in1=exp_half[:], op=ALU.pow
+            )
+            nc.gpsimd.tensor_scalar(
+                out=per_row("below", g)[:], in0=lengths[:, TG : 2 * TG], scalar1=1.0, scalar2=BAG_EPS,
+                op0=ALU.mult, op1=ALU.add,
+            )
+            nc.gpsimd.tensor_tensor(
+                out=per_row("inverse", g)[:], in0=per_row("below", g)[:], in1=exp_minus_one[:], op=ALU.pow
+            )
+            nc.gpsimd.tensor_tensor(
+                out=per_row("ratio", g)[:], in0=per_row("inverse", g)[:], in1=lengths[:, 0:TG], op=ALU.mult
+            )
+            nc.gpsimd.tensor_scalar(
+                out=per_row("alpha", g)[:], in0=per_row("ratio", g)[:], scalar1=1.0, scalar2=0.0,
+                op0=ALU.min, op1=ALU.max,
+            )
+
+        def shifted(g, t):
+            if not exists(g):
+                return
+            h_m = rows_back(g, t)
+            pre = work.tile([P, H], F32, name="pre", tag="pre", bufs=6)
+            live[("pre", g, t)] = pre
+            nc.vector.scalar_tensor_tensor(
+                out=pre[:], in0=h_m[:], scalar=per_row("alpha", g)[:, t : t + 1],
+                in1=live[("main", g)][:, t, :], op0=ALU.mult, op1=ALU.add,
+                accum_out=per_row("total", g)[:, t : t + 1],
+            )
+
+        def mean(g):
+            if not exists(g):
+                return
+            nc.vector.tensor_scalar_mul(out=per_row("mean", g)[:], in0=per_row("total", g)[:], scalar1=1.0 / H)
+
+        def variance(g, t):
+            if not exists(g):
+                return
+            nc.scalar.activation(
+                out=unread()[:], in_=live[("pre", g, t)][:], func=ACT.Square,
+                bias=per_row("mean", g)[:, t : t + 1], scale=-1.0,
+                accum_out=per_row("spread", g)[:, t : t + 1],
+            )
+
+        def centred(g, t):
+            if not exists(g):
+                return
+            scaled = work.tile([P, H], F32, name="scaled", tag="scaled", bufs=8)
+            live[("scaled", g, t)] = scaled
+            nc.vector.scalar_tensor_tensor(
+                out=scaled[:], in0=live[("pre", g, t)][:], scalar=per_row("mean", g)[:, t : t + 1],
+                in1=ln_g_all[:], op0=ALU.subtract, op1=ALU.mult,
+            )
+
+        def bag_over_std(g):
+            if not exists(g):
+                return
+            nc.gpsimd.tensor_scalar(
+                out=per_row("var", g)[:], in0=per_row("spread", g)[:], scalar1=1.0 / H, scalar2=LN_EPS,
+                op0=ALU.mult, op1=ALU.add,
+            )
+            nc.gpsimd.tensor_tensor(
+                out=per_row("rstd", g)[:], in0=per_row("var", g)[:], in1=exp_minus_half[:], op=ALU.pow
+            )
+            nc.gpsimd.tensor_tensor(
+                out=per_row("bag_rstd", g)[:], in0=per_row("rstd", g)[:], in1=bag[:, tiles_of(g)], op=ALU.mult
+            )
+
+        def carry(g, t):
+            if not exists(g):
+                return
+            j = g * TG + t
+            outer = bank([P, H])
+            nc.tensor.matmul(out=outer[:], lhsT=bag_diag[:, j, :], rhs=ln_b_all[:], start=True, stop=True)
+            if t % 2 == 0:
+                live[("shift_c", g, t // 2)] = work.tile([P, 2, H], F32, name="shift_c", tag="shift_c", bufs=6)
+            nc.vector.scalar_tensor_tensor(
+                out=live[("shift_c", g, t // 2)][:, t % 2, :], in0=live[("main", g)][:, t, :],
+                scalar=not_bag[:, j : j + 1], in1=outer[:], op0=ALU.mult, op1=ALU.add,
+            )
+
+        def blend(g, t):
+            if not exists(g):
+                return
+            shift_c = live[("shift_c", g, t // 2)]
+            nc.vector.scalar_tensor_tensor(
+                out=shift_c[:, t % 2, :], in0=live[("scaled", g, t)][:],
+                scalar=per_row("bag_rstd", g)[:, t : t + 1], in1=shift_c[:, t % 2, :],
+                op0=ALU.mult, op1=ALU.add,
+            )
+            if t % 2 == 1:
+                nc.sync.dma_start(out=shift_v[:, two_tiles_of(g, t // 2), :], in_=shift_c[:])
+
+        def gated_tanh(g, half):
+            if not exists(g):
+                return
+            h = work.tile([P, 2, H], F32, name="h", tag="h", bufs=4)
+            nc.scalar.activation(out=h[:], in_=live[("shift_c", g, half)][:], func=ACT.Tanh)
+            engine = nc.vector if g == GROUPS - 1 else nc.gpsimd
+            engine.tensor_tensor(
+                out=h[:], in0=h[:], in1=live[("o", g)][:, 2 * half : 2 * half + 2, :], op=ALU.mult
+            )
+            nc.sync.dma_start(out=h_v[:, two_tiles_of(g, half), :], in_=h[:])
+
+        for r in range(LAG_QUANTISE, GROUPS + LAG_OUT):
+            load_states(r - LAG_QUANTISE + LOAD_AHEAD)
+            load_o(r - LAG_OUT + LOAD_AHEAD)
+            for i in range(TG):
+                gate_sums(r, i)
+                gate_relu(r, i)
+                variance(r - LAG_STATS, i)
+                centred(r - LAG_STATS, i)
+                gate_product(r, i - 1)
+            gate_product(r, TG - 1)
+            bag_over_std(r - LAG_STATS)
+            for i in range(TG):
+                norms(r - LAG_NORM, i)
+                shifted(r - LAG_PRE, i)
+                blend(r - LAG_OUT, i)
+            alpha(r - LAG_NORM)
+            mean(r - LAG_PRE)
+            for i in range(TG):
+                carry(r - LAG_CARRY, i)
+                k_to_partitions(r - LAG_QUANTISE, i)
+                if i == 1:
+                    quantise(r - LAG_QUANTISE - 1, "branch")
+                if i == 3:
+                    quantise(r - LAG_QUANTISE, "main")
+                if i % 2 == 1:
+                    gated_tanh(r - LAG_OUT, i // 2)

@@ -16,22 +16,27 @@ P = 128
 ROWS = 4096
 H = 512
 TILES = ROWS // P
-TG = 4
+TG = 2
 GROUPS = TILES // TG
 GROUP_ROWS = TG * P
 CHUNKS = H // P
+STEP_CHUNKS = CHUNKS // TG
 LN_EPS = 1e-5
 BAG_EPS = 1e-6
 
 FLOPS = 2 * ROWS * (2 * H + H) * H
 
-LAG_QUANTISE = -2
-LAG_NORM = 1
-LAG_PRE = 2
-LAG_STATS = 3
-LAG_CARRY = 3
-LAG_OUT = 4
-LOAD_AHEAD = 1
+LAG_AHEAD = -1
+LAG_PRE = 1
+LAG_OUT = 2
+AHEAD_STATES = 2
+AHEAD_O = 1
+O_COLS = 256
+O_VECTOR = 1
+MAIN_BUFS = 8
+SHIFT_BUFS = 6
+O_BUFS = 4
+DIAG_STEP = 4
 
 
 def tile_bag_lstm_pb_t_kernel(
@@ -60,7 +65,7 @@ def tile_bag_lstm_pb_t_kernel(
 
         def per_row(name, g, width=TG):
             if (name, g) not in live:
-                live[(name, g)] = small.tile([P, width], F32, name=name, tag=name)
+                live[(name, g)] = small.tile([P, width], F32, name=name, tag=name, bufs=6)
             return live[(name, g)]
 
         def unread():
@@ -68,9 +73,6 @@ def tile_bag_lstm_pb_t_kernel(
 
         def tiles_of(g):
             return slice(g * TG, (g + 1) * TG)
-
-        def two_tiles_of(g, half):
-            return slice(g * TG + 2 * half, g * TG + 2 * half + 2)
 
         def exists(g):
             return 0 <= g < GROUPS
@@ -85,7 +87,7 @@ def tile_bag_lstm_pb_t_kernel(
         def load_states(g):
             if not exists(g):
                 return
-            live[("main", g)] = inputs.tile([P, TG, H], BF16, name="main_t", tag="main", bufs=7)
+            live[("main", g)] = inputs.tile([P, TG, H], BF16, name="main_t", tag="main", bufs=MAIN_BUFS)
             nc.sync.dma_start(out=live[("main", g)][:], in_=main_v[:, tiles_of(g), :])
             live[("branch", g)] = inputs.tile([P, TG, H], BF16, name="branch_t", tag="branch")
             nc.sync.dma_start(out=live[("branch", g)][:], in_=branch_v[:, tiles_of(g), :])
@@ -93,7 +95,7 @@ def tile_bag_lstm_pb_t_kernel(
         def load_o(g):
             if not exists(g):
                 return
-            live[("o", g)] = inputs.tile([P, TG, H], BF16, name="o_t", tag="o")
+            live[("o", g)] = inputs.tile([P, TG, H], BF16, name="o_t", tag="o", bufs=O_BUFS)
             nc.sync.dma_start(out=live[("o", g)][:], in_=o_v[:, tiles_of(g), :])
 
         w_rows = const.tile([P, 3, 4, H], BF16, name="w_rows")
@@ -106,7 +108,6 @@ def tile_bag_lstm_pb_t_kernel(
         ones_b = const.tile([P, P], BF16, name="ones_b")
         exp_half = const.tile([P, 2 * TG], F32, name="exp_half")
         exp_minus_half = const.tile([P, TG], F32, name="exp_minus_half")
-        exp_minus_one = const.tile([P, TG], F32, name="exp_minus_one")
         bias_rows = const.tile([P, P], BF16, name="bias_rows")
         ln_rows = const.tile([P, 2 * H], BF16, name="ln_rows")
         bag_b = const.tile([P, TILES], BF16, name="bag_b")
@@ -117,86 +118,82 @@ def tile_bag_lstm_pb_t_kernel(
         bag_diag = const.tile([P, TILES, P], BF16, name="bag_diag")
         ln_g_all = psum_g.tile([P, H], F32, name="ln_g_all")
 
-        for s in range(3):
-            load_weights(s)
-        for g in range(LOAD_AHEAD):
-            load_states(g)
-
-        nc.vector.memset(table_warm[:], 0.0)
+        load_states(0)
         nc.scalar.dma_start(out=bag_b[:], in_=is_bag.rearrange("(p j) one -> p (j one)", j=TILES))
-        nc.vector.memset(bias_rows[:].bitcast(I32), 0)
-        nc.scalar.dma_start(out=bias_rows[0:CHUNKS, :], in_=b_mb.rearrange("(a x) -> a x", x=P))
-        nc.scalar.dma_start(out=bias_rows[CHUNKS : 2 * CHUNKS, :], in_=b_b.rearrange("(a x) -> a x", x=P))
+        nc.vector.memset(table_warm[:], 0.0)
         nc.vector.memset(ln_rows[:].bitcast(I32), 0)
+        nc.vector.memset(bias_rows[:].bitcast(I32), 0)
         nc.scalar.dma_start(out=ln_rows[0:1, 0:H], in_=ln_g.unsqueeze(0))
         nc.scalar.dma_start(out=ln_rows[0:1, H : 2 * H], in_=ln_b.unsqueeze(0))
+        nc.scalar.dma_start(out=bias_rows[0:CHUNKS, :], in_=b_mb.rearrange("(a x) -> a x", x=P))
+        nc.scalar.dma_start(out=bias_rows[CHUNKS : 2 * CHUNKS, :], in_=b_b.rearrange("(a x) -> a x", x=P))
+        for s in range(3):
+            load_weights(s)
         nc.scalar.activation(out=table_warm[:], in_=table_warm[:], func=ACT.Tanh)
         masks.make_identity(nc, ident_f[:])
         masks.make_identity(nc, ident_b[:])
         nc.vector.memset(ones_b[:], 1.0)
         nc.vector.memset(exp_half[:], 0.5)
         nc.vector.memset(exp_minus_half[:], -0.5)
-        nc.vector.memset(exp_minus_one[:], -1.0)
         nc.vector.tensor_copy(out=bag[:], in_=bag_b[:])
         nc.vector.tensor_scalar(
             out=not_bag[:], in0=bag_b[:], scalar1=-1.0, scalar2=1.0, op0=ALU.mult, op1=ALU.add
         )
-        bias_t = bank([P, P], BF16)
-        nc.tensor.transpose(bias_t[:], bias_rows[:], ident_b[:])
-        nc.vector.tensor_copy(out=bias_cols[:], in_=bias_t[:, 0 : 2 * CHUNKS])
-        nc.tensor.matmul(out=ln_g_all[:], lhsT=ones_b[:], rhs=ln_rows[:, 0:H], start=True, stop=True)
-        ln_b_bank = bank([P, H])
-        nc.tensor.matmul(out=ln_b_bank[:], lhsT=ones_b[:], rhs=ln_rows[:, H : 2 * H], start=True, stop=True)
-        nc.vector.tensor_copy(out=ln_b_all[:], in_=ln_b_bank[:])
-        for first in range(0, TILES, 8):
-            some = slice(first, first + 8)
-            nc.gpsimd.tensor_tensor(
-                out=bag_diag[:, some, :], in0=ident_b[:].unsqueeze(1).to_broadcast([P, 8, P]),
-                in1=bag_b[:, some].unsqueeze(2).to_broadcast([P, 8, P]), op=ALU.mult,
-            )
 
-        def group_weights(s, engine):
-            dst = w_grouped[:, s].rearrange("p (a i) v -> p a v i", i=4)
-            src = w_rows[:, s].rearrange("p v (a i) -> p a v i", i=4)
+        def bag_diagonals(r):
+            for j in range(DIAG_STEP * r, min(DIAG_STEP * (r + 1), TILES)):
+                nc.gpsimd.tensor_scalar(
+                    out=bag_diag[:, j, :], in0=ident_b[:], scalar1=bag[:, j : j + 1], scalar2=0.0,
+                    op0=ALU.mult, op1=ALU.add,
+                )
+
+        def spread_ln():
+            ln_b_bank = bank([P, H])
+            nc.tensor.matmul(out=ln_b_bank[:], lhsT=ones_b[:], rhs=ln_rows[:, H : 2 * H], start=True, stop=True)
+            nc.vector.tensor_copy(out=ln_b_all[:], in_=ln_b_bank[:])
+            nc.tensor.matmul(out=ln_g_all[:], lhsT=ones_b[:], rhs=ln_rows[:, 0:H], start=True, stop=True)
+
+        def spread_biases():
+            bias_t = bank([P, P], BF16)
+            nc.tensor.transpose(bias_t[:], bias_rows[:], ident_b[:])
+            nc.vector.tensor_copy(out=bias_cols[:], in_=bias_t[:, 0 : 2 * CHUNKS])
+
+        def group_weights(s, half, engine):
+            cols = slice(half * H // 2, (half + 1) * H // 2)
+            dst = w_grouped[:, s, cols, :].rearrange("p (a i) v -> p a v i", i=4)
+            src = w_rows[:, s, :, cols].rearrange("p v (a i) -> p a v i", i=4)
             if engine == "scalar":
                 nc.scalar.copy(out=dst, in_=src)
             else:
                 nc.vector.tensor_copy(out=dst, in_=src)
 
-        def quantise_weights(s):
+        def quantise_weights(s, half):
+            cols = slice(half * H // 2, (half + 1) * H // 2)
             nc.vector.quantize_mx(
-                out=w_words[:, s, :].bitcast(FP8X4),
-                scales=w_scales[:, s, :],
-                in_=w_grouped[:, s].rearrange("p n v -> p (n v)"),
+                out=w_words[:, s, cols].bitcast(FP8X4),
+                scales=w_scales[:, s, cols],
+                in_=w_grouped[:, s, cols, :].rearrange("p n v -> p (n v)"),
             )
-
-        group_weights(0, "vector")
-        group_weights(1, "scalar")
-        group_weights(2, "vector")
-        for s in range(3):
-            quantise_weights(s)
 
         def k_to_partitions(g, i):
             if not exists(g):
                 return
-            which = "main" if i < 2 else "branch"
-            half = i % 2
+            which = "main" if i == 0 else "branch"
             pairs = live[(which, g)][:].bitcast(F32)
             turned = bank([P, 2, 2 * P])
             for t in range(2):
                 for u in range(2):
                     nc.tensor.transpose(
                         turned[:, u, t * P : (t + 1) * P],
-                        pairs[:, 2 * half + t, u : 2 * P : 2],
+                        pairs[:, t, u : 2 * P : 2],
                         ident_f[:],
                     )
-            if half == 0:
-                live[(which + "_k", g)] = work.tile(
-                    [P, 4 * GROUP_ROWS], BF16, name=which + "_k", tag=which + "_k", bufs=2, align_bytes=64
-                )
+            live[(which + "_k", g)] = work.tile(
+                [P, 4 * GROUP_ROWS], BF16, name=which + "_k", tag=which + "_k", bufs=2, align_bytes=64
+            )
             grouped = live[(which + "_k", g)][:].bitcast(F32).rearrange("p (row u) -> p row u", u=2)
             nc.scalar.copy(
-                out=grouped[:, half * 2 * P : (half + 1) * 2 * P, :],
+                out=grouped,
                 in_=turned[:].rearrange("p u row -> p row u"),
             )
 
@@ -210,49 +207,56 @@ def tile_bag_lstm_pb_t_kernel(
             )
             live[(which + "_q", g)] = (words_q, scales_q)
 
-        def gate_sums(g, c):
+        def gate_sums(g, i):
             if not exists(g):
                 return
             main_w, main_s = live[("main_q", g)]
             branch_w, branch_s = live[("branch_q", g)]
-            cols = slice(c * P, (c + 1) * P)
-            sum_mb = bank([P, GROUP_ROWS])
-            nc.tensor.matmul_mx(
-                out=sum_mb[:], lhsT=w_words[:, 0, cols].bitcast(FP8X4), lhsT_scale=w_scales[:, 0, cols],
-                rhs=main_w[:].bitcast(FP8X4), rhs_scale=main_s[:], start=True, stop=False,
-            )
-            nc.tensor.matmul_mx(
-                out=sum_mb[:], lhsT=w_words[:, 1, cols].bitcast(FP8X4), lhsT_scale=w_scales[:, 1, cols],
-                rhs=branch_w[:].bitcast(FP8X4), rhs_scale=branch_s[:], start=False, stop=True,
-            )
-            sum_b = bank([P, GROUP_ROWS])
-            nc.tensor.matmul_mx(
-                out=sum_b[:], lhsT=w_words[:, 2, cols].bitcast(FP8X4), lhsT_scale=w_scales[:, 2, cols],
-                rhs=branch_w[:].bitcast(FP8X4), rhs_scale=branch_s[:], start=True, stop=True,
-            )
-            live[("sum_mb", g, c)] = sum_mb
-            live[("sum_b", g, c)] = sum_b
+            sum_mb = bank([P, STEP_CHUNKS, GROUP_ROWS])
+            sum_b = bank([P, STEP_CHUNKS, GROUP_ROWS])
+            for a in range(STEP_CHUNKS):
+                cols = slice((i * STEP_CHUNKS + a) * P, (i * STEP_CHUNKS + a + 1) * P)
+                nc.tensor.matmul_mx(
+                    out=sum_mb[:, a, :], lhsT=w_words[:, 0, cols].bitcast(FP8X4), lhsT_scale=w_scales[:, 0, cols],
+                    rhs=main_w[:].bitcast(FP8X4), rhs_scale=main_s[:], start=True, stop=False,
+                )
+                nc.tensor.matmul_mx(
+                    out=sum_mb[:, a, :], lhsT=w_words[:, 1, cols].bitcast(FP8X4), lhsT_scale=w_scales[:, 1, cols],
+                    rhs=branch_w[:].bitcast(FP8X4), rhs_scale=branch_s[:], start=False, stop=True,
+                )
+            for a in range(STEP_CHUNKS):
+                cols = slice((i * STEP_CHUNKS + a) * P, (i * STEP_CHUNKS + a + 1) * P)
+                nc.tensor.matmul_mx(
+                    out=sum_b[:, a, :], lhsT=w_words[:, 2, cols].bitcast(FP8X4), lhsT_scale=w_scales[:, 2, cols],
+                    rhs=branch_w[:].bitcast(FP8X4), rhs_scale=branch_s[:], start=True, stop=True,
+                )
+            live[("sum_mb", g, i)] = sum_mb
+            live[("sum_b", g, i)] = sum_b
 
-        def gate_relu(g, c):
+        def gate_relu(g, i):
             if not exists(g):
                 return
-            weight_b = work.tile([P, GROUP_ROWS], F32, name="weight_b", tag="weight_b")
-            live[("weight_b", g, c)] = weight_b
-            nc.scalar.activation(
-                out=weight_b[:], in_=live[("sum_mb", g, c)][:], func=ACT.Relu,
-                bias=bias_cols[:, c : c + 1], scale=1.0,
-            )
+            weight_b = work.tile([P, STEP_CHUNKS, GROUP_ROWS], F32, name="weight_b", tag="weight_b")
+            live[("weight_b", g, i)] = weight_b
+            for a in range(STEP_CHUNKS):
+                c = i * STEP_CHUNKS + a
+                nc.scalar.activation(
+                    out=weight_b[:, a, :], in_=live[("sum_mb", g, i)][:, a, :], func=ACT.Relu,
+                    bias=bias_cols[:, c : c + 1], scale=1.0,
+                )
 
-        def gate_product(g, c):
-            if not exists(g) or c < 0:
+        def gate_product(g, i):
+            if not exists(g) or i < 0:
                 return
-            if c == 0:
+            if i == 0:
                 live[("h_m_t", g)] = work.tile([P, CHUNKS, GROUP_ROWS], F32, name="h_m_t", tag="h_m_t")
-            nc.vector.scalar_tensor_tensor(
-                out=live[("h_m_t", g)][:, c, :], in0=live[("sum_b", g, c)][:],
-                scalar=bias_cols[:, CHUNKS + c : CHUNKS + c + 1], in1=live[("weight_b", g, c)][:],
-                op0=ALU.add, op1=ALU.mult,
-            )
+            for a in range(STEP_CHUNKS):
+                c = i * STEP_CHUNKS + a
+                nc.vector.scalar_tensor_tensor(
+                    out=live[("h_m_t", g)][:, c, :], in0=live[("sum_b", g, i)][:, a, :],
+                    scalar=bias_cols[:, CHUNKS + c : CHUNKS + c + 1], in1=live[("weight_b", g, i)][:, a, :],
+                    op0=ALU.add, op1=ALU.mult,
+                )
 
         def rows_back(g, t):
             h_m = bank([P, H])
@@ -262,46 +266,52 @@ def tile_bag_lstm_pb_t_kernel(
                 )
             return h_m
 
-        def norms(g, t):
+        def square_main(g, t):
             if not exists(g):
                 return
-            squares = per_row("squares", g, 2 * TG)
-            h_m = rows_back(g, t)
             nc.scalar.activation(
                 out=unread()[:], in_=live[("main", g)][:, t, :], func=ACT.Square,
-                accum_out=squares[:, t : t + 1],
-            )
-            nc.scalar.activation(
-                out=unread()[:], in_=h_m[:], func=ACT.Square, accum_out=squares[:, TG + t : TG + t + 1]
+                accum_out=per_row("squares", g, 2 * TG)[:, t : t + 1],
             )
 
-        def alpha(g):
+        def square_h_m(g, t):
+            if not exists(g):
+                return
+            h_m = rows_back(g, t)
+            nc.scalar.activation(
+                out=unread()[:], in_=h_m[:], func=ACT.Square,
+                accum_out=per_row("squares", g, 2 * TG)[:, TG + t : TG + t + 1],
+            )
+
+        def lengths(g):
+            if not exists(g):
+                return
+            nc.gpsimd.tensor_tensor(
+                out=per_row("lengths", g, 2 * TG)[:], in0=per_row("squares", g, 2 * TG)[:], in1=exp_half[:],
+                op=ALU.pow,
+            )
+
+        def alpha(g, part):
             if not exists(g):
                 return
             lengths = per_row("lengths", g, 2 * TG)
-            nc.gpsimd.tensor_tensor(
-                out=lengths[:], in0=per_row("squares", g, 2 * TG)[:], in1=exp_half[:], op=ALU.pow
-            )
-            nc.gpsimd.tensor_scalar(
-                out=per_row("below", g)[:], in0=lengths[:, TG : 2 * TG], scalar1=1.0, scalar2=BAG_EPS,
-                op0=ALU.mult, op1=ALU.add,
-            )
-            nc.gpsimd.tensor_tensor(
-                out=per_row("inverse", g)[:], in0=per_row("below", g)[:], in1=exp_minus_one[:], op=ALU.pow
-            )
-            nc.gpsimd.tensor_tensor(
-                out=per_row("ratio", g)[:], in0=per_row("inverse", g)[:], in1=lengths[:, 0:TG], op=ALU.mult
-            )
-            nc.gpsimd.tensor_scalar(
-                out=per_row("alpha", g)[:], in0=per_row("ratio", g)[:], scalar1=1.0, scalar2=0.0,
-                op0=ALU.min, op1=ALU.max,
-            )
+            if part == 0:
+                nc.vector.scalar_tensor_tensor(
+                    out=per_row("below", g)[:], in0=lengths[:, TG : 2 * TG], scalar=BAG_EPS, in1=lengths[:, 0:TG],
+                    op0=ALU.add, op1=ALU.max,
+                )
+            elif part == 1:
+                nc.vector.reciprocal(out=per_row("inverse", g)[:], in_=per_row("below", g)[:])
+            else:
+                nc.vector.tensor_tensor(
+                    out=per_row("alpha", g)[:], in0=per_row("inverse", g)[:], in1=lengths[:, 0:TG], op=ALU.mult
+                )
 
         def shifted(g, t):
             if not exists(g):
                 return
             h_m = rows_back(g, t)
-            pre = work.tile([P, H], F32, name="pre", tag="pre", bufs=6)
+            pre = work.tile([P, H], F32, name="pre", tag="pre", bufs=4)
             live[("pre", g, t)] = pre
             nc.vector.scalar_tensor_tensor(
                 out=pre[:], in0=h_m[:], scalar=per_row("alpha", g)[:, t : t + 1],
@@ -326,7 +336,7 @@ def tile_bag_lstm_pb_t_kernel(
         def centred(g, t):
             if not exists(g):
                 return
-            scaled = work.tile([P, H], F32, name="scaled", tag="scaled", bufs=8)
+            scaled = work.tile([P, H], F32, name="scaled", tag="scaled", bufs=4)
             live[("scaled", g, t)] = scaled
             nc.vector.scalar_tensor_tensor(
                 out=scaled[:], in0=live[("pre", g, t)][:], scalar=per_row("mean", g)[:, t : t + 1],
@@ -347,65 +357,109 @@ def tile_bag_lstm_pb_t_kernel(
                 out=per_row("bag_rstd", g)[:], in0=per_row("rstd", g)[:], in1=bag[:, tiles_of(g)], op=ALU.mult
             )
 
+        def carry_outer(g, t):
+            if not exists(g):
+                return
+            live[("outer", g, t)] = bank([P, H])
+            nc.tensor.matmul(
+                out=live[("outer", g, t)][:], lhsT=bag_diag[:, g * TG + t, :], rhs=ln_b_all[:], start=True, stop=True
+            )
+
         def carry(g, t):
             if not exists(g):
                 return
             j = g * TG + t
-            outer = bank([P, H])
-            nc.tensor.matmul(out=outer[:], lhsT=bag_diag[:, j, :], rhs=ln_b_all[:], start=True, stop=True)
-            if t % 2 == 0:
-                live[("shift_c", g, t // 2)] = work.tile([P, 2, H], F32, name="shift_c", tag="shift_c", bufs=6)
+            if t == 0:
+                live[("shift_c", g)] = work.tile([P, 2, H], F32, name="shift_c", tag="shift_c", bufs=SHIFT_BUFS)
             nc.vector.scalar_tensor_tensor(
-                out=live[("shift_c", g, t // 2)][:, t % 2, :], in0=live[("main", g)][:, t, :],
-                scalar=not_bag[:, j : j + 1], in1=outer[:], op0=ALU.mult, op1=ALU.add,
+                out=live[("shift_c", g)][:, t, :], in0=live[("main", g)][:, t, :],
+                scalar=not_bag[:, j : j + 1], in1=live[("outer", g, t)][:], op0=ALU.mult, op1=ALU.add,
             )
 
         def blend(g, t):
             if not exists(g):
                 return
-            shift_c = live[("shift_c", g, t // 2)]
+            shift_c = live[("shift_c", g)]
             nc.vector.scalar_tensor_tensor(
-                out=shift_c[:, t % 2, :], in0=live[("scaled", g, t)][:],
-                scalar=per_row("bag_rstd", g)[:, t : t + 1], in1=shift_c[:, t % 2, :],
+                out=shift_c[:, t, :], in0=live[("scaled", g, t)][:],
+                scalar=per_row("bag_rstd", g)[:, t : t + 1], in1=shift_c[:, t, :],
                 op0=ALU.mult, op1=ALU.add,
             )
-            if t % 2 == 1:
-                nc.sync.dma_start(out=shift_v[:, two_tiles_of(g, t // 2), :], in_=shift_c[:])
+            if t == TG - 1:
+                nc.sync.dma_start(out=shift_v[:, tiles_of(g), :], in_=shift_c[:])
 
-        def gated_tanh(g, half):
+        def gated_tanh(g):
             if not exists(g):
                 return
-            h = work.tile([P, 2, H], F32, name="h", tag="h", bufs=4)
-            nc.scalar.activation(out=h[:], in_=live[("shift_c", g, half)][:], func=ACT.Tanh)
-            engine = nc.vector if g == GROUPS - 1 else nc.gpsimd
-            engine.tensor_tensor(
-                out=h[:], in0=h[:], in1=live[("o", g)][:, 2 * half : 2 * half + 2, :], op=ALU.mult
-            )
-            nc.sync.dma_start(out=h_v[:, two_tiles_of(g, half), :], in_=h[:])
+            h = work.tile([P, TG, H], F32, name="h", tag="h", bufs=4)
+            nc.scalar.activation(out=h[:], in_=live[("shift_c", g)][:], func=ACT.Tanh)
+            engine = nc.vector if g >= GROUPS - O_VECTOR else nc.gpsimd
+            for t in range(TG):
+                for first in range(0, H, O_COLS):
+                    some = slice(first, first + O_COLS)
+                    engine.tensor_tensor(
+                        out=h[:, t, some], in0=h[:, t, some], in1=live[("o", g)][:, t, some], op=ALU.mult
+                    )
+            nc.sync.dma_start(out=h_v[:, tiles_of(g), :], in_=h[:])
 
-        for r in range(LAG_QUANTISE, GROUPS + LAG_OUT):
-            load_states(r - LAG_QUANTISE + LOAD_AHEAD)
-            load_o(r - LAG_OUT + LOAD_AHEAD)
-            for i in range(TG):
-                gate_sums(r, i)
-                gate_relu(r, i)
-                variance(r - LAG_STATS, i)
-                centred(r - LAG_STATS, i)
-                gate_product(r, i - 1)
-            gate_product(r, TG - 1)
-            bag_over_std(r - LAG_STATS)
-            for i in range(TG):
-                norms(r - LAG_NORM, i)
-                shifted(r - LAG_PRE, i)
-                blend(r - LAG_OUT, i)
-            alpha(r - LAG_NORM)
-            mean(r - LAG_PRE)
-            for i in range(TG):
-                carry(r - LAG_CARRY, i)
-                k_to_partitions(r - LAG_QUANTISE, i)
-                if i == 1:
-                    quantise(r - LAG_QUANTISE - 1, "branch")
-                if i == 3:
-                    quantise(r - LAG_QUANTISE, "main")
-                if i % 2 == 1:
-                    gated_tanh(r - LAG_OUT, i // 2)
+        load_states(1)
+        bag_diagonals(0)
+        k_to_partitions(0, 0)
+        k_to_partitions(0, 1)
+        group_weights(0, 0, "vector")
+        quantise(0, "main")
+        group_weights(0, 1, "vector")
+        quantise(0, "branch")
+        quantise_weights(0, 0)
+        group_weights(1, 0, "scalar")
+        spread_ln()
+        spread_biases()
+        square_main(0, 0)
+        square_main(0, 1)
+        group_weights(2, 0, "vector")
+        quantise_weights(1, 0)
+        group_weights(1, 1, "scalar")
+        quantise_weights(2, 0)
+        group_weights(2, 1, "vector")
+        quantise_weights(0, 1)
+        quantise_weights(1, 1)
+        quantise_weights(2, 1)
+        for g in range(2, 1 + AHEAD_STATES):
+            load_states(g)
+        for r in range(0, GROUPS + 3):
+            load_states(r + 1 + AHEAD_STATES)
+            load_o(r - 2 + AHEAD_O)
+            carry_outer(r, 0)
+            carry(r, 0)
+            alpha(r - 1, 0)
+            gate_sums(r, 0)
+            gate_relu(r, 0)
+            k_to_partitions(r + 1, 0)
+            gate_product(r, 0)
+            alpha(r - 1, 1)
+            carry_outer(r, 1)
+            carry(r, 1)
+            alpha(r - 1, 2)
+            gate_sums(r, 1)
+            gate_relu(r, 1)
+            k_to_partitions(r + 1, 1)
+            gate_product(r, 1)
+            shifted(r - 1, 0)
+            square_main(r + 1, 0)
+            shifted(r - 1, 1)
+            square_main(r + 1, 1)
+            quantise(r + 1, "main")
+            mean(r - 1)
+            square_h_m(r, 0)
+            square_h_m(r, 1)
+            lengths(r)
+            blend(r - 2, 0)
+            blend(r - 2, 1)
+            quantise(r + 1, "branch")
+            variance(r - 1, 0)
+            centred(r - 1, 0)
+            variance(r - 1, 1)
+            centred(r - 1, 1)
+            bag_over_std(r - 1)
+            bag_diagonals(r + 1)
+            gated_tanh(r - 2)

@@ -31,7 +31,7 @@ LAG_PRE = 1
 LAG_OUT = 2
 AHEAD_STATES = 2
 AHEAD_O = 1
-O_COLS = 256
+O_COLS = 512
 O_VECTOR = 1
 MAIN_BUFS = 8
 SHIFT_BUFS = 6
@@ -142,9 +142,8 @@ def tile_bag_lstm_pb_t_kernel(
 
         def bag_diagonals(r):
             for j in range(DIAG_STEP * r, min(DIAG_STEP * (r + 1), TILES)):
-                nc.gpsimd.tensor_scalar(
-                    out=bag_diag[:, j, :], in0=ident_b[:], scalar1=bag[:, j : j + 1], scalar2=0.0,
-                    op0=ALU.mult, op1=ALU.add,
+                nc.vector.tensor_scalar(
+                    out=bag_diag[:, j, :], in0=ident_b[:], scalar1=bag[:, j : j + 1], scalar2=None, op0=ALU.mult
                 )
 
         def spread_ln():
@@ -188,24 +187,28 @@ def tile_bag_lstm_pb_t_kernel(
                         pairs[:, t, u : 2 * P : 2],
                         ident_f[:],
                     )
-            live[(which + "_k", g)] = work.tile(
-                [P, 4 * GROUP_ROWS], BF16, name=which + "_k", tag=which + "_k", bufs=2, align_bytes=64
-            )
-            grouped = live[(which + "_k", g)][:].bitcast(F32).rearrange("p (row u) -> p row u", u=2)
+            if i == 0:
+                live[("states_k", g)] = work.tile(
+                    [P, 2, 4 * GROUP_ROWS], BF16, name="states_k", tag="states_k", bufs=2, align_bytes=64
+                )
+            grouped = live[("states_k", g)][:, i, :].bitcast(F32).rearrange("p (row u) -> p row u", u=2)
             nc.scalar.copy(
                 out=grouped,
                 in_=turned[:].rearrange("p u row -> p row u"),
             )
 
-        def quantise(g, which):
+        def quantise(g):
             if not exists(g):
                 return
-            words_q = work.tile([P, GROUP_ROWS], U32, name=which + "_w", tag=which + "_w", align_bytes=64)
-            scales_q = work.tile([P, GROUP_ROWS], U8, name=which + "_s", tag=which + "_s", align_bytes=64)
+            words_q = work.tile([P, 2, GROUP_ROWS], U32, name="states_w", tag="states_w", align_bytes=64)
+            scales_q = work.tile([P, 2, GROUP_ROWS], U8, name="states_s", tag="states_s", align_bytes=64)
             nc.vector.quantize_mx(
-                out=words_q[:].bitcast(FP8X4), scales=scales_q[:], in_=live[(which + "_k", g)][:]
+                out=words_q[:].rearrange("p s row -> p (s row)").bitcast(FP8X4),
+                scales=scales_q[:].rearrange("p s row -> p (s row)"),
+                in_=live[("states_k", g)][:].rearrange("p s k -> p (s k)"),
             )
-            live[(which + "_q", g)] = (words_q, scales_q)
+            live[("main_q", g)] = (words_q[:, 0, :], scales_q[:, 0, :])
+            live[("branch_q", g)] = (words_q[:, 1, :], scales_q[:, 1, :])
 
         def gate_sums(g, i):
             if not exists(g):
@@ -218,17 +221,17 @@ def tile_bag_lstm_pb_t_kernel(
                 cols = slice((i * STEP_CHUNKS + a) * P, (i * STEP_CHUNKS + a + 1) * P)
                 nc.tensor.matmul_mx(
                     out=sum_mb[:, a, :], lhsT=w_words[:, 0, cols].bitcast(FP8X4), lhsT_scale=w_scales[:, 0, cols],
-                    rhs=main_w[:].bitcast(FP8X4), rhs_scale=main_s[:], start=True, stop=False,
+                    rhs=main_w.bitcast(FP8X4), rhs_scale=main_s, start=True, stop=False,
                 )
                 nc.tensor.matmul_mx(
                     out=sum_mb[:, a, :], lhsT=w_words[:, 1, cols].bitcast(FP8X4), lhsT_scale=w_scales[:, 1, cols],
-                    rhs=branch_w[:].bitcast(FP8X4), rhs_scale=branch_s[:], start=False, stop=True,
+                    rhs=branch_w.bitcast(FP8X4), rhs_scale=branch_s, start=False, stop=True,
                 )
             for a in range(STEP_CHUNKS):
                 cols = slice((i * STEP_CHUNKS + a) * P, (i * STEP_CHUNKS + a + 1) * P)
                 nc.tensor.matmul_mx(
                     out=sum_b[:, a, :], lhsT=w_words[:, 2, cols].bitcast(FP8X4), lhsT_scale=w_scales[:, 2, cols],
-                    rhs=branch_w[:].bitcast(FP8X4), rhs_scale=branch_s[:], start=True, stop=True,
+                    rhs=branch_w.bitcast(FP8X4), rhs_scale=branch_s, start=True, stop=True,
                 )
             live[("sum_mb", g, i)] = sum_mb
             live[("sum_b", g, i)] = sum_b
@@ -303,7 +306,7 @@ def tile_bag_lstm_pb_t_kernel(
             elif part == 1:
                 nc.vector.reciprocal(out=per_row("inverse", g)[:], in_=per_row("below", g)[:])
             else:
-                nc.vector.tensor_tensor(
+                nc.gpsimd.tensor_tensor(
                     out=per_row("alpha", g)[:], in0=per_row("inverse", g)[:], in1=lengths[:, 0:TG], op=ALU.mult
                 )
 
@@ -407,9 +410,8 @@ def tile_bag_lstm_pb_t_kernel(
         k_to_partitions(0, 0)
         k_to_partitions(0, 1)
         group_weights(0, 0, "vector")
-        quantise(0, "main")
         group_weights(0, 1, "vector")
-        quantise(0, "branch")
+        quantise(0)
         quantise_weights(0, 0)
         group_weights(1, 0, "scalar")
         spread_ln()
@@ -431,15 +433,12 @@ def tile_bag_lstm_pb_t_kernel(
             load_o(r - 2 + AHEAD_O)
             carry_outer(r, 0)
             carry(r, 0)
-            alpha(r - 1, 0)
             gate_sums(r, 0)
             gate_relu(r, 0)
             k_to_partitions(r + 1, 0)
             gate_product(r, 0)
-            alpha(r - 1, 1)
             carry_outer(r, 1)
             carry(r, 1)
-            alpha(r - 1, 2)
             gate_sums(r, 1)
             gate_relu(r, 1)
             k_to_partitions(r + 1, 1)
@@ -448,18 +447,20 @@ def tile_bag_lstm_pb_t_kernel(
             square_main(r + 1, 0)
             shifted(r - 1, 1)
             square_main(r + 1, 1)
-            quantise(r + 1, "main")
+            quantise(r + 1)
             mean(r - 1)
             square_h_m(r, 0)
             square_h_m(r, 1)
             lengths(r)
             blend(r - 2, 0)
             blend(r - 2, 1)
-            quantise(r + 1, "branch")
             variance(r - 1, 0)
             centred(r - 1, 0)
+            alpha(r, 0)
             variance(r - 1, 1)
             centred(r - 1, 1)
+            alpha(r, 1)
             bag_over_std(r - 1)
+            alpha(r, 2)
             bag_diagonals(r + 1)
             gated_tanh(r - 2)

@@ -30,9 +30,7 @@ LAG_AHEAD = -1
 LAG_PRE = 1
 LAG_OUT = 2
 AHEAD_STATES = 2
-AHEAD_O = 1
-O_COLS = 512
-O_VECTOR = 1
+AHEAD_O = 2
 MAIN_BUFS = 8
 SHIFT_BUFS = 6
 O_BUFS = 4
@@ -118,17 +116,18 @@ def tile_bag_lstm_pb_t_kernel(
         bag_diag = const.tile([P, TILES, P], BF16, name="bag_diag")
         ln_g_all = psum_g.tile([P, H], F32, name="ln_g_all")
 
-        load_states(0)
-        nc.scalar.dma_start(out=bag_b[:], in_=is_bag.rearrange("(p j) one -> p (j one)", j=TILES))
         nc.vector.memset(table_warm[:], 0.0)
         nc.vector.memset(ln_rows[:].bitcast(I32), 0)
         nc.vector.memset(bias_rows[:].bitcast(I32), 0)
-        nc.scalar.dma_start(out=ln_rows[0:1, 0:H], in_=ln_g.unsqueeze(0))
-        nc.scalar.dma_start(out=ln_rows[0:1, H : 2 * H], in_=ln_b.unsqueeze(0))
-        nc.scalar.dma_start(out=bias_rows[0:CHUNKS, :], in_=b_mb.rearrange("(a x) -> a x", x=P))
-        nc.scalar.dma_start(out=bias_rows[CHUNKS : 2 * CHUNKS, :], in_=b_b.rearrange("(a x) -> a x", x=P))
-        for s in range(3):
-            load_weights(s)
+        nc.sync.dma_start(out=bag_b[:], in_=is_bag.rearrange("(p j) one -> p (j one)", j=TILES))
+        load_states(0)
+        load_weights(0)
+        nc.sync.dma_start(out=bias_rows[0:CHUNKS, :], in_=b_mb.rearrange("(a x) -> a x", x=P))
+        load_weights(1)
+        nc.sync.dma_start(out=bias_rows[CHUNKS : 2 * CHUNKS, :], in_=b_b.rearrange("(a x) -> a x", x=P))
+        load_weights(2)
+        nc.sync.dma_start(out=ln_rows[0:1, H : 2 * H], in_=ln_b.unsqueeze(0))
+        nc.sync.dma_start(out=ln_rows[0:1, 0:H], in_=ln_g.unsqueeze(0))
         nc.scalar.activation(out=table_warm[:], in_=table_warm[:], func=ACT.Tanh)
         masks.make_identity(nc, ident_f[:])
         masks.make_identity(nc, ident_b[:])
@@ -149,7 +148,7 @@ def tile_bag_lstm_pb_t_kernel(
         def spread_ln():
             ln_b_bank = bank([P, H])
             nc.tensor.matmul(out=ln_b_bank[:], lhsT=ones_b[:], rhs=ln_rows[:, H : 2 * H], start=True, stop=True)
-            nc.vector.tensor_copy(out=ln_b_all[:], in_=ln_b_bank[:])
+            nc.scalar.copy(out=ln_b_all[:], in_=ln_b_bank[:])
             nc.tensor.matmul(out=ln_g_all[:], lhsT=ones_b[:], rhs=ln_rows[:, 0:H], start=True, stop=True)
 
         def spread_biases():
@@ -322,10 +321,13 @@ def tile_bag_lstm_pb_t_kernel(
                 accum_out=per_row("total", g)[:, t : t + 1],
             )
 
-        def mean(g):
+        def mean(g, t=None):
             if not exists(g):
                 return
-            nc.vector.tensor_scalar_mul(out=per_row("mean", g)[:], in0=per_row("total", g)[:], scalar1=1.0 / H)
+            some = slice(0, TG) if t is None else slice(t, t + 1)
+            nc.vector.tensor_scalar_mul(
+                out=per_row("mean", g)[:, some], in0=per_row("total", g)[:, some], scalar1=1.0 / H
+            )
 
         def variance(g, t):
             if not exists(g):
@@ -346,18 +348,20 @@ def tile_bag_lstm_pb_t_kernel(
                 in1=ln_g_all[:], op0=ALU.subtract, op1=ALU.mult,
             )
 
-        def bag_over_std(g):
+        def bag_over_std(g, t=None):
             if not exists(g):
                 return
+            some = slice(0, TG) if t is None else slice(t, t + 1)
+            tiles = slice(g * TG + some.start, g * TG + some.stop)
             nc.gpsimd.tensor_scalar(
-                out=per_row("var", g)[:], in0=per_row("spread", g)[:], scalar1=1.0 / H, scalar2=LN_EPS,
+                out=per_row("var", g)[:, some], in0=per_row("spread", g)[:, some], scalar1=1.0 / H, scalar2=LN_EPS,
                 op0=ALU.mult, op1=ALU.add,
             )
             nc.gpsimd.tensor_tensor(
-                out=per_row("rstd", g)[:], in0=per_row("var", g)[:], in1=exp_minus_half[:], op=ALU.pow
+                out=per_row("rstd", g)[:, some], in0=per_row("var", g)[:, some], in1=exp_minus_half[:, some], op=ALU.pow
             )
             nc.gpsimd.tensor_tensor(
-                out=per_row("bag_rstd", g)[:], in0=per_row("rstd", g)[:], in1=bag[:, tiles_of(g)], op=ALU.mult
+                out=per_row("bag_rstd", g)[:, some], in0=per_row("rstd", g)[:, some], in1=bag[:, tiles], op=ALU.mult
             )
 
         def carry_outer(g, t):
@@ -388,22 +392,33 @@ def tile_bag_lstm_pb_t_kernel(
                 scalar=per_row("bag_rstd", g)[:, t : t + 1], in1=shift_c[:, t, :],
                 op0=ALU.mult, op1=ALU.add,
             )
-            if t == TG - 1:
-                nc.sync.dma_start(out=shift_v[:, tiles_of(g), :], in_=shift_c[:])
 
-        def gated_tanh(g):
+        def store_shift(g, t=None):
             if not exists(g):
                 return
-            h = work.tile([P, TG, H], F32, name="h", tag="h", bufs=4)
-            nc.scalar.activation(out=h[:], in_=live[("shift_c", g)][:], func=ACT.Tanh)
-            engine = nc.vector if g >= GROUPS - O_VECTOR else nc.gpsimd
-            for t in range(TG):
-                for first in range(0, H, O_COLS):
-                    some = slice(first, first + O_COLS)
-                    engine.tensor_tensor(
-                        out=h[:, t, some], in0=h[:, t, some], in1=live[("o", g)][:, t, some], op=ALU.mult
-                    )
-            nc.sync.dma_start(out=h_v[:, tiles_of(g), :], in_=h[:])
+            some = slice(0, TG) if t is None else slice(t, t + 1)
+            tiles = slice(g * TG + some.start, g * TG + some.stop)
+            nc.sync.dma_start(out=shift_v[:, tiles, :], in_=live[("shift_c", g)][:, some, :])
+
+        def tanh(g, t=None):
+            if not exists(g):
+                return
+            some = slice(0, TG) if t is None else slice(t, t + 1)
+            if ("h", g) not in live:
+                live[("h", g)] = work.tile([P, TG, H], F32, name="h", tag="h", bufs=4)
+            nc.scalar.activation(out=live[("h", g)][:, some, :], in_=live[("shift_c", g)][:, some, :], func=ACT.Tanh)
+
+        def gate_tanh(g, engine, t=None):
+            if not exists(g):
+                return
+            h = live[("h", g)]
+            some = slice(0, TG) if t is None else slice(t, t + 1)
+            tiles = slice(g * TG + some.start, g * TG + some.stop)
+            for a in range(some.start, some.stop):
+                engine.tensor_tensor(
+                    out=h[:, a, :], in0=h[:, a, :], in1=live[("o", g)][:, a, :], op=ALU.mult
+                )
+            nc.sync.dma_start(out=h_v[:, tiles, :], in_=h[:, some, :])
 
         load_states(1)
         bag_diagonals(0)
@@ -414,21 +429,21 @@ def tile_bag_lstm_pb_t_kernel(
         quantise(0)
         quantise_weights(0, 0)
         group_weights(1, 0, "scalar")
-        spread_ln()
+        group_weights(2, 0, "vector")
+        group_weights(1, 1, "scalar")
+        quantise_weights(1, 0)
+        group_weights(2, 1, "vector")
+        quantise_weights(2, 0)
         spread_biases()
+        spread_ln()
         square_main(0, 0)
         square_main(0, 1)
-        group_weights(2, 0, "vector")
-        quantise_weights(1, 0)
-        group_weights(1, 1, "scalar")
-        quantise_weights(2, 0)
-        group_weights(2, 1, "vector")
         quantise_weights(0, 1)
         quantise_weights(1, 1)
         quantise_weights(2, 1)
         for g in range(2, 1 + AHEAD_STATES):
             load_states(g)
-        for r in range(0, GROUPS + 3):
+        for r in range(0, GROUPS):
             load_states(r + 1 + AHEAD_STATES)
             load_o(r - 2 + AHEAD_O)
             carry_outer(r, 0)
@@ -446,14 +461,15 @@ def tile_bag_lstm_pb_t_kernel(
             shifted(r - 1, 0)
             square_main(r + 1, 0)
             shifted(r - 1, 1)
-            square_main(r + 1, 1)
             quantise(r + 1)
             mean(r - 1)
             square_h_m(r, 0)
             square_h_m(r, 1)
+            square_main(r + 1, 1)
             lengths(r)
             blend(r - 2, 0)
             blend(r - 2, 1)
+            store_shift(r - 2)
             variance(r - 1, 0)
             centred(r - 1, 0)
             alpha(r, 0)
@@ -463,4 +479,29 @@ def tile_bag_lstm_pb_t_kernel(
             bag_over_std(r - 1)
             alpha(r, 2)
             bag_diagonals(r + 1)
-            gated_tanh(r - 2)
+            tanh(r - 2)
+            gate_tanh(r - 2, nc.gpsimd if r < GROUPS - 1 else nc.vector)
+        last = GROUPS - 1
+        shifted(last, 0)
+        shifted(last, 1)
+        mean(last, 0)
+        variance(last, 0)
+        bag_over_std(last, 0)
+        blend(last - 1, 0)
+        mean(last, 1)
+        variance(last, 1)
+        bag_over_std(last, 1)
+        blend(last - 1, 1)
+        store_shift(last - 1)
+        tanh(last - 1)
+        centred(last, 0)
+        centred(last, 1)
+        blend(last, 0)
+        store_shift(last, 0)
+        tanh(last, 0)
+        gate_tanh(last - 1, nc.vector)
+        blend(last, 1)
+        store_shift(last, 1)
+        tanh(last, 1)
+        gate_tanh(last, nc.vector, 0)
+        gate_tanh(last, nc.vector, 1)

@@ -34,7 +34,6 @@ AHEAD_O = 2
 MAIN_BUFS = 8
 SHIFT_BUFS = 6
 O_BUFS = 4
-DIAG_STEP = 4
 
 
 def tile_bag_lstm_pb_t_kernel(
@@ -139,9 +138,9 @@ def tile_bag_lstm_pb_t_kernel(
             out=not_bag[:], in0=bag_b[:], scalar1=-1.0, scalar2=1.0, op0=ALU.mult, op1=ALU.add
         )
 
-        def bag_diagonals(r):
-            for j in range(DIAG_STEP * r, min(DIAG_STEP * (r + 1), TILES)):
-                nc.vector.tensor_scalar(
+        def bag_diagonals(engine, first, last):
+            for j in range(first, last):
+                engine.tensor_scalar(
                     out=bag_diag[:, j, :], in0=ident_b[:], scalar1=bag[:, j : j + 1], scalar2=None, op0=ALU.mult
                 )
 
@@ -173,7 +172,7 @@ def tile_bag_lstm_pb_t_kernel(
                 in_=w_grouped[:, s, cols, :].rearrange("p n v -> p (n v)"),
             )
 
-        def k_to_partitions(g, i):
+        def k_turn(g, i):
             if not exists(g):
                 return
             which = "main" if i == 0 else "branch"
@@ -186,6 +185,12 @@ def tile_bag_lstm_pb_t_kernel(
                         pairs[:, t, u : 2 * P : 2],
                         ident_f[:],
                     )
+            live[("turned", g, i)] = turned
+
+        def k_copy(g, i):
+            if not exists(g):
+                return
+            turned = live[("turned", g, i)]
             if i == 0:
                 live[("states_k", g)] = work.tile(
                     [P, 2, 4 * GROUP_ROWS], BF16, name="states_k", tag="states_k", bufs=2, align_bytes=64
@@ -214,8 +219,14 @@ def tile_bag_lstm_pb_t_kernel(
                 return
             main_w, main_s = live[("main_q", g)]
             branch_w, branch_s = live[("branch_q", g)]
-            sum_mb = bank([P, STEP_CHUNKS, GROUP_ROWS])
             sum_b = bank([P, STEP_CHUNKS, GROUP_ROWS])
+            sum_mb = bank([P, STEP_CHUNKS, GROUP_ROWS])
+            for a in range(STEP_CHUNKS):
+                cols = slice((i * STEP_CHUNKS + a) * P, (i * STEP_CHUNKS + a + 1) * P)
+                nc.tensor.matmul_mx(
+                    out=sum_b[:, a, :], lhsT=w_words[:, 2, cols].bitcast(FP8X4), lhsT_scale=w_scales[:, 2, cols],
+                    rhs=branch_w.bitcast(FP8X4), rhs_scale=branch_s, start=True, stop=True,
+                )
             for a in range(STEP_CHUNKS):
                 cols = slice((i * STEP_CHUNKS + a) * P, (i * STEP_CHUNKS + a + 1) * P)
                 nc.tensor.matmul_mx(
@@ -225,12 +236,6 @@ def tile_bag_lstm_pb_t_kernel(
                 nc.tensor.matmul_mx(
                     out=sum_mb[:, a, :], lhsT=w_words[:, 1, cols].bitcast(FP8X4), lhsT_scale=w_scales[:, 1, cols],
                     rhs=branch_w.bitcast(FP8X4), rhs_scale=branch_s, start=False, stop=True,
-                )
-            for a in range(STEP_CHUNKS):
-                cols = slice((i * STEP_CHUNKS + a) * P, (i * STEP_CHUNKS + a + 1) * P)
-                nc.tensor.matmul_mx(
-                    out=sum_b[:, a, :], lhsT=w_words[:, 2, cols].bitcast(FP8X4), lhsT_scale=w_scales[:, 2, cols],
-                    rhs=branch_w.bitcast(FP8X4), rhs_scale=branch_s, start=True, stop=True,
                 )
             live[("sum_mb", g, i)] = sum_mb
             live[("sum_b", g, i)] = sum_b
@@ -305,9 +310,11 @@ def tile_bag_lstm_pb_t_kernel(
             elif part == 1:
                 nc.vector.reciprocal(out=per_row("inverse", g)[:], in_=per_row("below", g)[:])
             else:
-                nc.gpsimd.tensor_tensor(
-                    out=per_row("alpha", g)[:], in0=per_row("inverse", g)[:], in1=lengths[:, 0:TG], op=ALU.mult
-                )
+                for t in range(TG):
+                    nc.vector.tensor_scalar(
+                        out=per_row("alpha", g)[:, t : t + 1], in0=per_row("inverse", g)[:, t : t + 1],
+                        scalar1=lengths[:, t : t + 1], scalar2=None, op0=ALU.mult,
+                    )
 
         def shifted(g, t):
             if not exists(g):
@@ -421,9 +428,11 @@ def tile_bag_lstm_pb_t_kernel(
             nc.sync.dma_start(out=h_v[:, tiles, :], in_=h[:, some, :])
 
         load_states(1)
-        bag_diagonals(0)
-        k_to_partitions(0, 0)
-        k_to_partitions(0, 1)
+        bag_diagonals(nc.vector, 0, 4)
+        k_turn(0, 0)
+        k_copy(0, 0)
+        k_turn(0, 1)
+        k_copy(0, 1)
         group_weights(0, 0, "vector")
         group_weights(0, 1, "vector")
         quantise(0)
@@ -448,21 +457,27 @@ def tile_bag_lstm_pb_t_kernel(
             load_o(r - 2 + AHEAD_O)
             carry_outer(r, 0)
             carry(r, 0)
+            alpha(r - 1, 1)
             gate_sums(r, 0)
             gate_relu(r, 0)
-            k_to_partitions(r + 1, 0)
+            k_turn(r + 1, 0)
+            k_copy(r + 1, 0)
             gate_product(r, 0)
+            alpha(r - 1, 2)
             carry_outer(r, 1)
             carry(r, 1)
             gate_sums(r, 1)
             gate_relu(r, 1)
-            k_to_partitions(r + 1, 1)
+            k_turn(r + 1, 1)
+            k_copy(r + 1, 1)
             gate_product(r, 1)
             shifted(r - 1, 0)
             square_main(r + 1, 0)
             shifted(r - 1, 1)
             quantise(r + 1)
             mean(r - 1)
+            if r == 0:
+                bag_diagonals(nc.vector, 4, TILES)
             square_h_m(r, 0)
             square_h_m(r, 1)
             square_main(r + 1, 1)
@@ -472,16 +487,15 @@ def tile_bag_lstm_pb_t_kernel(
             store_shift(r - 2)
             variance(r - 1, 0)
             centred(r - 1, 0)
-            alpha(r, 0)
             variance(r - 1, 1)
             centred(r - 1, 1)
-            alpha(r, 1)
+            alpha(r, 0)
             bag_over_std(r - 1)
-            alpha(r, 2)
-            bag_diagonals(r + 1)
             tanh(r - 2)
             gate_tanh(r - 2, nc.gpsimd if r < GROUPS - 1 else nc.vector)
         last = GROUPS - 1
+        alpha(last, 1)
+        alpha(last, 2)
         shifted(last, 0)
         shifted(last, 1)
         mean(last, 0)

@@ -32,7 +32,7 @@ LAG_OUT = 2
 AHEAD_STATES = 2
 AHEAD_O = 2
 MAIN_BUFS = 8
-SHIFT_BUFS = 6
+SHIFT_BUFS = GROUPS
 O_BUFS = 4
 
 
@@ -193,7 +193,7 @@ def tile_bag_lstm_pb_t_kernel(
             turned = live[("turned", g, i)]
             if i == 0:
                 live[("states_k", g)] = work.tile(
-                    [P, 2, 4 * GROUP_ROWS], BF16, name="states_k", tag="states_k", bufs=2, align_bytes=64
+                    [P, 2, 4 * GROUP_ROWS], BF16, name="states_k", tag="states_k", bufs=3, align_bytes=64
                 )
             grouped = live[("states_k", g)][:, i, :].bitcast(F32).rearrange("p (row u) -> p row u", u=2)
             nc.scalar.copy(
@@ -265,13 +265,15 @@ def tile_bag_lstm_pb_t_kernel(
                     op0=ALU.add, op1=ALU.mult,
                 )
 
-        def rows_back(g, t):
+        def rows_back(g, t, use):
+            if not exists(g):
+                return
             h_m = bank([P, H])
+            live[(use, g, t)] = h_m
             for c in range(CHUNKS):
                 nc.tensor.transpose(
                     h_m[:, c * P : (c + 1) * P], live[("h_m_t", g)][:, c, t * P : (t + 1) * P], ident_f[:]
                 )
-            return h_m
 
         def square_main(g, t):
             if not exists(g):
@@ -284,42 +286,45 @@ def tile_bag_lstm_pb_t_kernel(
         def square_h_m(g, t):
             if not exists(g):
                 return
-            h_m = rows_back(g, t)
+            h_m = live[("to_square", g, t)]
             nc.scalar.activation(
                 out=unread()[:], in_=h_m[:], func=ACT.Square,
                 accum_out=per_row("squares", g, 2 * TG)[:, TG + t : TG + t + 1],
             )
 
-        def lengths(g):
+        def lengths(g, t=None):
             if not exists(g):
                 return
+            some = slice(0, 2 * TG) if t is None else slice(t, 2 * TG, TG)
+            count = 2 * TG if t is None else 2
             nc.gpsimd.tensor_tensor(
-                out=per_row("lengths", g, 2 * TG)[:], in0=per_row("squares", g, 2 * TG)[:], in1=exp_half[:],
-                op=ALU.pow,
+                out=per_row("lengths", g, 2 * TG)[:, some], in0=per_row("squares", g, 2 * TG)[:, some],
+                in1=exp_half[:, 0:count], op=ALU.pow,
             )
 
-        def alpha(g, part):
+        def alpha(g, part, t=None):
             if not exists(g):
                 return
             lengths = per_row("lengths", g, 2 * TG)
+            some = slice(0, TG) if t is None else slice(t, t + 1)
             if part == 0:
                 nc.vector.scalar_tensor_tensor(
-                    out=per_row("below", g)[:], in0=lengths[:, TG : 2 * TG], scalar=BAG_EPS, in1=lengths[:, 0:TG],
-                    op0=ALU.add, op1=ALU.max,
+                    out=per_row("below", g)[:, some], in0=lengths[:, TG + some.start : TG + some.stop], scalar=BAG_EPS,
+                    in1=lengths[:, some], op0=ALU.add, op1=ALU.max,
                 )
             elif part == 1:
-                nc.vector.reciprocal(out=per_row("inverse", g)[:], in_=per_row("below", g)[:])
+                nc.vector.reciprocal(out=per_row("inverse", g)[:, some], in_=per_row("below", g)[:, some])
             else:
-                for t in range(TG):
-                    nc.vector.tensor_scalar(
-                        out=per_row("alpha", g)[:, t : t + 1], in0=per_row("inverse", g)[:, t : t + 1],
-                        scalar1=lengths[:, t : t + 1], scalar2=None, op0=ALU.mult,
+                for a in range(some.start, some.stop):
+                    nc.scalar.activation(
+                        out=per_row("alpha", g)[:, a : a + 1], in_=per_row("inverse", g)[:, a : a + 1],
+                        func=ACT.Copy, scale=lengths[:, a : a + 1],
                     )
 
         def shifted(g, t):
             if not exists(g):
                 return
-            h_m = rows_back(g, t)
+            h_m = live[("to_shift", g, t)]
             pre = work.tile([P, H], F32, name="pre", tag="pre", bufs=4)
             live[("pre", g, t)] = pre
             nc.vector.scalar_tensor_tensor(
@@ -437,24 +442,26 @@ def tile_bag_lstm_pb_t_kernel(
         group_weights(0, 1, "vector")
         quantise(0)
         quantise_weights(0, 0)
+        quantise_weights(0, 1)
         group_weights(1, 0, "scalar")
-        group_weights(2, 0, "vector")
         group_weights(1, 1, "scalar")
         quantise_weights(1, 0)
-        group_weights(2, 1, "vector")
+        group_weights(2, 0, "vector")
+        quantise_weights(1, 1)
+        group_weights(2, 1, "scalar")
         quantise_weights(2, 0)
         spread_biases()
         spread_ln()
         square_main(0, 0)
         square_main(0, 1)
-        quantise_weights(0, 1)
-        quantise_weights(1, 1)
         quantise_weights(2, 1)
         for g in range(2, 1 + AHEAD_STATES):
             load_states(g)
-        for r in range(0, GROUPS):
+        for r in range(0, GROUPS - 1):
             load_states(r + 1 + AHEAD_STATES)
             load_o(r - 2 + AHEAD_O)
+            if r == GROUPS - 2:
+                load_o(GROUPS - 1)
             carry_outer(r, 0)
             carry(r, 0)
             alpha(r - 1, 1)
@@ -471,14 +478,18 @@ def tile_bag_lstm_pb_t_kernel(
             k_turn(r + 1, 1)
             k_copy(r + 1, 1)
             gate_product(r, 1)
+            rows_back(r - 1, 0, "to_shift")
             shifted(r - 1, 0)
             square_main(r + 1, 0)
+            rows_back(r - 1, 1, "to_shift")
             shifted(r - 1, 1)
             quantise(r + 1)
             mean(r - 1)
             if r == 0:
                 bag_diagonals(nc.vector, 4, TILES)
+            rows_back(r, 0, "to_square")
             square_h_m(r, 0)
+            rows_back(r, 1, "to_square")
             square_h_m(r, 1)
             square_main(r + 1, 1)
             lengths(r)
@@ -492,19 +503,57 @@ def tile_bag_lstm_pb_t_kernel(
             alpha(r, 0)
             bag_over_std(r - 1)
             tanh(r - 2)
-            gate_tanh(r - 2, nc.gpsimd if r < GROUPS - 1 else nc.vector)
+            gate_tanh(r - 2, nc.gpsimd)
         last = GROUPS - 1
-        alpha(last, 1)
-        alpha(last, 2)
+        carry_outer(last, 0)
+        carry_outer(last, 1)
+        gate_sums(last, 0)
+        gate_relu(last, 0)
+        alpha(last - 1, 1)
+        carry(last, 0)
+        gate_product(last, 0)
+        gate_sums(last, 1)
+        gate_relu(last, 1)
+        alpha(last - 1, 2)
+        gate_product(last, 1)
+        rows_back(last - 1, 0, "to_shift")
+        rows_back(last, 0, "to_square")
+        rows_back(last, 1, "to_square")
+        rows_back(last - 1, 1, "to_shift")
+        shifted(last - 1, 0)
+        shifted(last - 1, 1)
+        square_h_m(last, 0)
+        lengths(last, 0)
+        square_h_m(last, 1)
+        lengths(last, 1)
+        carry(last, 1)
+        mean(last - 1)
+        variance(last - 1, 0)
+        variance(last - 1, 1)
+        alpha(last, 0, 0)
+        blend(last - 2, 0)
+        alpha(last, 1, 0)
+        blend(last - 2, 1)
+        store_shift(last - 2)
+        alpha(last, 2, 0)
+        alpha(last, 0, 1)
+        bag_over_std(last - 1)
+        rows_back(last, 0, "to_shift")
+        rows_back(last, 1, "to_shift")
         shifted(last, 0)
-        shifted(last, 1)
+        alpha(last, 1, 1)
         mean(last, 0)
+        alpha(last, 2, 1)
+        shifted(last, 1)
         variance(last, 0)
         bag_over_std(last, 0)
-        blend(last - 1, 0)
+        centred(last - 1, 0)
         mean(last, 1)
         variance(last, 1)
         bag_over_std(last, 1)
+        tanh(last - 2)
+        centred(last - 1, 1)
+        blend(last - 1, 0)
         blend(last - 1, 1)
         store_shift(last - 1)
         tanh(last - 1)
@@ -513,9 +562,10 @@ def tile_bag_lstm_pb_t_kernel(
         blend(last, 0)
         store_shift(last, 0)
         tanh(last, 0)
-        gate_tanh(last - 1, nc.vector)
+        gate_tanh(last - 2, nc.vector)
         blend(last, 1)
         store_shift(last, 1)
         tanh(last, 1)
+        gate_tanh(last - 1, nc.vector)
         gate_tanh(last, nc.vector, 0)
         gate_tanh(last, nc.vector, 1)

@@ -62,7 +62,7 @@ def tile_bag_lstm_pb_t_kernel(
 
         def per_row(name, g, width=TG):
             if (name, g) not in live:
-                live[(name, g)] = small.tile([P, width], F32, name=name, tag=name, bufs=6)
+                live[(name, g)] = small.tile([P, width], F32, name=name, tag=name, bufs=GROUPS)
             return live[(name, g)]
 
         def unread():
@@ -121,11 +121,11 @@ def tile_bag_lstm_pb_t_kernel(
         nc.sync.dma_start(out=bag_b[:], in_=is_bag.rearrange("(p j) one -> p (j one)", j=TILES))
         load_states(0)
         load_weights(0)
+        nc.sync.dma_start(out=ln_rows[0:1, H : 2 * H], in_=ln_b.unsqueeze(0))
         nc.sync.dma_start(out=bias_rows[0:CHUNKS, :], in_=b_mb.rearrange("(a x) -> a x", x=P))
         load_weights(1)
         nc.sync.dma_start(out=bias_rows[CHUNKS : 2 * CHUNKS, :], in_=b_b.rearrange("(a x) -> a x", x=P))
         load_weights(2)
-        nc.sync.dma_start(out=ln_rows[0:1, H : 2 * H], in_=ln_b.unsqueeze(0))
         nc.sync.dma_start(out=ln_rows[0:1, 0:H], in_=ln_g.unsqueeze(0))
         nc.scalar.activation(out=table_warm[:], in_=table_warm[:], func=ACT.Tanh)
         masks.make_identity(nc, ident_f[:])
@@ -144,25 +144,24 @@ def tile_bag_lstm_pb_t_kernel(
                     out=bag_diag[:, j, :], in0=ident_b[:], scalar1=bag[:, j : j + 1], scalar2=None, op0=ALU.mult
                 )
 
-        def spread_ln():
+        def spread_ln_b():
             ln_b_bank = bank([P, H])
             nc.tensor.matmul(out=ln_b_bank[:], lhsT=ones_b[:], rhs=ln_rows[:, H : 2 * H], start=True, stop=True)
             nc.scalar.copy(out=ln_b_all[:], in_=ln_b_bank[:])
+
+        def spread_ln_g():
             nc.tensor.matmul(out=ln_g_all[:], lhsT=ones_b[:], rhs=ln_rows[:, 0:H], start=True, stop=True)
 
         def spread_biases():
             bias_t = bank([P, P], BF16)
             nc.tensor.transpose(bias_t[:], bias_rows[:], ident_b[:])
-            nc.vector.tensor_copy(out=bias_cols[:], in_=bias_t[:, 0 : 2 * CHUNKS])
+            nc.scalar.copy(out=bias_cols[:], in_=bias_t[:, 0 : 2 * CHUNKS])
 
-        def group_weights(s, half, engine):
+        def group_weights(s, half):
             cols = slice(half * H // 2, (half + 1) * H // 2)
             dst = w_grouped[:, s, cols, :].rearrange("p (a i) v -> p a v i", i=4)
             src = w_rows[:, s, :, cols].rearrange("p v (a i) -> p a v i", i=4)
-            if engine == "scalar":
-                nc.scalar.copy(out=dst, in_=src)
-            else:
-                nc.vector.tensor_copy(out=dst, in_=src)
+            nc.vector.tensor_copy(out=dst, in_=src)
 
         def quantise_weights(s, half):
             cols = slice(half * H // 2, (half + 1) * H // 2)
@@ -417,7 +416,7 @@ def tile_bag_lstm_pb_t_kernel(
                 return
             some = slice(0, TG) if t is None else slice(t, t + 1)
             if ("h", g) not in live:
-                live[("h", g)] = work.tile([P, TG, H], F32, name="h", tag="h", bufs=4)
+                live[("h", g)] = work.tile([P, TG, H], F32, name="h", tag="h", bufs=8)
             nc.scalar.activation(out=live[("h", g)][:, some, :], in_=live[("shift_c", g)][:, some, :], func=ACT.Tanh)
 
         def gate_tanh(g, engine, t=None):
@@ -438,22 +437,22 @@ def tile_bag_lstm_pb_t_kernel(
         k_copy(0, 0)
         k_turn(0, 1)
         k_copy(0, 1)
-        group_weights(0, 0, "vector")
-        group_weights(0, 1, "vector")
-        quantise(0)
-        quantise_weights(0, 0)
-        quantise_weights(0, 1)
-        group_weights(1, 0, "scalar")
-        group_weights(1, 1, "scalar")
-        quantise_weights(1, 0)
-        group_weights(2, 0, "vector")
-        quantise_weights(1, 1)
-        group_weights(2, 1, "scalar")
-        quantise_weights(2, 0)
+        spread_ln_b()
         spread_biases()
-        spread_ln()
+        group_weights(0, 0)
+        group_weights(0, 1)
+        quantise(0)
+        group_weights(1, 0)
+        quantise_weights(0, 0)
+        group_weights(2, 0)
+        quantise_weights(1, 0)
+        quantise_weights(2, 0)
         square_main(0, 0)
         square_main(0, 1)
+        group_weights(1, 1)
+        group_weights(2, 1)
+        quantise_weights(0, 1)
+        quantise_weights(1, 1)
         quantise_weights(2, 1)
         for g in range(2, 1 + AHEAD_STATES):
             load_states(g)
@@ -486,6 +485,7 @@ def tile_bag_lstm_pb_t_kernel(
             quantise(r + 1)
             mean(r - 1)
             if r == 0:
+                spread_ln_g()
                 bag_diagonals(nc.vector, 4, TILES)
             rows_back(r, 0, "to_square")
             square_h_m(r, 0)
@@ -517,9 +517,9 @@ def tile_bag_lstm_pb_t_kernel(
         alpha(last - 1, 2)
         gate_product(last, 1)
         rows_back(last - 1, 0, "to_shift")
+        rows_back(last - 1, 1, "to_shift")
         rows_back(last, 0, "to_square")
         rows_back(last, 1, "to_square")
-        rows_back(last - 1, 1, "to_shift")
         shifted(last - 1, 0)
         shifted(last - 1, 1)
         square_h_m(last, 0)

@@ -425,10 +425,9 @@ def tile_bag_lstm_pb_t_kernel(
             h = live[("h", g)]
             some = slice(0, TG) if t is None else slice(t, t + 1)
             tiles = slice(g * TG + some.start, g * TG + some.stop)
-            for a in range(some.start, some.stop):
-                engine.tensor_tensor(
-                    out=h[:, a, :], in0=h[:, a, :], in1=live[("o", g)][:, a, :], op=ALU.mult
-                )
+            engine.tensor_tensor(
+                out=h[:, some, :], in0=h[:, some, :], in1=live[("o", g)][:, some, :], op=ALU.mult
+            )
             nc.sync.dma_start(out=h_v[:, tiles, :], in_=h[:, some, :])
 
         load_states(1)

from contextlib import ExitStack

import concourse.masks as masks
import concourse.mybir as mybir

F32 = mybir.dt.float32
BF16 = mybir.dt.bfloat16
U8 = mybir.dt.uint8
U32 = mybir.dt.uint32
I32 = mybir.dt.int32
FP8X4 = mybir.dt.float8_e4m3fn_x4
ALU = mybir.AluOpType
ACT = mybir.ActivationFunctionType

P = 128
ROWS = 4096
H = 512
TILES = ROWS // P
TG = 2
GROUPS = TILES // TG
GROUP_ROWS = TG * P
CHUNKS = H // P
STEP_CHUNKS = CHUNKS // TG
LN_EPS = 1e-5
BAG_EPS = 1e-6

FLOPS = 2 * ROWS * (2 * H + H) * H

LAG_AHEAD = -1
LAG_PRE = 1
LAG_OUT = 2
AHEAD_STATES = 2
AHEAD_O = 2
MAIN_BUFS = 8
SHIFT_BUFS = GROUPS
O_BUFS = 4


def tile_bag_lstm_pb_t_kernel(
    tc, main, branch, o, is_bag, W_mb, b_mb, W_b, b_b, ln_g, ln_b, out_0, out_1
):
    nc = tc.nc
    main_v = main.rearrange("(p j) col -> p j col", j=TILES)
    branch_v = branch.rearrange("(p j) col -> p j col", j=TILES)
    o_v = o.rearrange("(p j) col -> p j col", j=TILES)
    h_v = out_0.rearrange("(p j) col -> p j col", j=TILES)
    shift_v = out_1.rearrange("(p j) col -> p j col", j=TILES)

    with ExitStack() as ctx:
        const = ctx.enter_context(tc.tile_pool(name="const", bufs=1))
        inputs = ctx.enter_context(tc.tile_pool(name="inputs", bufs=3))
        work = ctx.enter_context(tc.tile_pool(name="work", bufs=3))
        small = ctx.enter_context(tc.tile_pool(name="small", bufs=3))
        psum_g = ctx.enter_context(tc.psum_pool(name="psum_g", bufs=1))
        psum = ctx.enter_context(tc.psum_pool(name="psum", bufs=7))
        ctx.enter_context(tc.manual_schedule())

        live = {}

        def bank(shape, dtype=F32):
            return psum.tile(shape, dtype, name="bank", tag="bank")

        def per_row(name, g, width=TG):
            if (name, g) not in live:
                live[(name, g)] = small.tile([P, width], F32, name=name, tag=name, bufs=GROUPS)
            return live[(name, g)]

        def unread():
            return work.tile([P, H], BF16, name="unread", tag="unread", bufs=4)

        def tiles_of(g):
            return slice(g * TG, (g + 1) * TG)

        def exists(g):
            return 0 <= g < GROUPS

        def load_weights(s):
            if s < 2:
                rows = W_mb.rearrange("(s p v) n -> s p v n", s=2, p=P, v=4)[s]
            else:
                rows = W_b.rearrange("(p v) n -> p v n", p=P, v=4)
            nc.sync.dma_start(out=w_rows[:, s], in_=rows)

        def load_states(g):
            if not exists(g):
                return
            live[("main", g)] = inputs.tile([P, TG, H], BF16, name="main_t", tag="main", bufs=MAIN_BUFS)
            nc.sync.dma_start(out=live[("main", g)][:], in_=main_v[:, tiles_of(g), :])
            live[("branch", g)] = inputs.tile([P, TG, H], BF16, name="branch_t", tag="branch")
            nc.sync.dma_start(out=live[("branch", g)][:], in_=branch_v[:, tiles_of(g), :])

        def load_o(g):
            if not exists(g):
                return
            live[("o", g)] = inputs.tile([P, TG, H], BF16, name="o_t", tag="o", bufs=O_BUFS)
            nc.sync.dma_start(out=live[("o", g)][:], in_=o_v[:, tiles_of(g), :])

        w_rows = const.tile([P, 3, 4, H], BF16, name="w_rows")
        w_grouped = const.tile([P, 3, H, 4], BF16, name="w_grouped", align_bytes=64)
        w_words = const.tile([P, 3, H], U32, name="w_words", align_bytes=64)
        w_scales = const.tile([P, 3, H], U8, name="w_scales", align_bytes=64)
        table_warm = const.tile([P, 1], F32, name="table_warm")
        ident_f = const.tile([P, P], F32, name="ident_f")
        ident_b = const.tile([P, P], BF16, name="ident_b")
        ones_b = const.tile([P, P], BF16, name="ones_b")
        exp_half = const.tile([P, 2 * TG], F32, name="exp_half")
        exp_minus_half = const.tile([P, TG], F32, name="exp_minus_half")
        bias_rows = const.tile([P, P], BF16, name="bias_rows")
        ln_rows = const.tile([P, 2 * H], BF16, name="ln_rows")
        bag_b = const.tile([P, TILES], BF16, name="bag_b")
        bag = const.tile([P, TILES], F32, name="bag")
        not_bag = const.tile([P, TILES], F32, name="not_bag")
        bias_cols = const.tile([P, 2 * CHUNKS], F32, name="bias_cols")
        ln_b_all = const.tile([P, H], BF16, name="ln_b_all")
        bag_diag = const.tile([P, TILES, P], BF16, name="bag_diag")
        ln_g_all = psum_g.tile([P, H], F32, name="ln_g_all")

        nc.vector.memset(table_warm[:], 0.0)
        nc.vector.memset(ln_rows[:].bitcast(I32), 0)
        nc.vector.memset(bias_rows[:].bitcast(I32), 0)
        nc.sync.dma_start(out=bag_b[:], in_=is_bag.rearrange("(p j) one -> p (j one)", j=TILES))
        load_states(0)
        load_weights(0)
        nc.sync.dma_start(out=ln_rows[0:1, H : 2 * H], in_=ln_b.unsqueeze(0))
        nc.sync.dma_start(out=bias_rows[0:CHUNKS, :], in_=b_mb.rearrange("(a x) -> a x", x=P))
        load_weights(1)
        nc.sync.dma_start(out=bias_rows[CHUNKS : 2 * CHUNKS, :], in_=b_b.rearrange("(a x) -> a x", x=P))
        load_weights(2)
        nc.sync.dma_start(out=ln_rows[0:1, 0:H], in_=ln_g.unsqueeze(0))
        nc.scalar.activation(out=table_warm[:], in_=table_warm[:], func=ACT.Tanh)
        masks.make_identity(nc, ident_f[:])
        masks.make_identity(nc, ident_b[:])
        nc.vector.memset(ones_b[:], 1.0)
        nc.vector.memset(exp_half[:], 0.5)
        nc.vector.memset(exp_minus_half[:], -0.5)
        nc.vector.tensor_copy(out=bag[:], in_=bag_b[:])
        nc.vector.tensor_scalar(
            out=not_bag[:], in0=bag_b[:], scalar1=-1.0, scalar2=1.0, op0=ALU.mult, op1=ALU.add
        )

        def bag_diagonals(engine, first, last):
            for j in range(first, last):
                engine.tensor_scalar(
                    out=bag_diag[:, j, :], in0=ident_b[:], scalar1=bag[:, j : j + 1], scalar2=None, op0=ALU.mult
                )

        def spread_ln_b():
            ln_b_bank = bank([P, H])
            nc.tensor.matmul(out=ln_b_bank[:], lhsT=ones_b[:], rhs=ln_rows[:, H : 2 * H], start=True, stop=True)
            nc.scalar.copy(out=ln_b_all[:], in_=ln_b_bank[:])

        def spread_ln_g():
            nc.tensor.matmul(out=ln_g_all[:], lhsT=ones_b[:], rhs=ln_rows[:, 0:H], start=True, stop=True)

        def spread_biases():
            bias_t = bank([P, P], BF16)
            nc.tensor.transpose(bias_t[:], bias_rows[:], ident_b[:])
            nc.scalar.copy(out=bias_cols[:], in_=bias_t[:, 0 : 2 * CHUNKS])

        def group_weights(s, half):
            cols = slice(half * H // 2, (half + 1) * H // 2)
            dst = w_grouped[:, s, cols, :].rearrange("p (a i) v -> p a v i", i=4)
            src = w_rows[:, s, :, cols].rearrange("p v (a i) -> p a v i", i=4)
            nc.vector.tensor_copy(out=dst, in_=src)

        def quantise_weights(s, half):
            cols = slice(half * H // 2, (half + 1) * H // 2)
            nc.vector.quantize_mx(
                out=w_words[:, s, cols].bitcast(FP8X4),
                scales=w_scales[:, s, cols],
                in_=w_grouped[:, s, cols, :].rearrange("p n v -> p (n v)"),
            )

        def k_turn(g, i):
            if not exists(g):
                return
            which = "main" if i == 0 else "branch"
            pairs = live[(which, g)][:].bitcast(F32)
            turned = bank([P, 2, 2 * P])
            for t in range(2):
                for u in range(2):
                    nc.tensor.transpose(
                        turned[:, u, t * P : (t + 1) * P],
                        pairs[:, t, u : 2 * P : 2],
                        ident_f[:],
                    )
            live[("turned", g, i)] = turned

        def k_copy(g, i):
            if not exists(g):
                return
            turned = live[("turned", g, i)]
            if i == 0:
                live[("states_k", g)] = work.tile(
                    [P, 2, 4 * GROUP_ROWS], BF16, name="states_k", tag="states_k", bufs=3, align_bytes=64
                )
            grouped = live[("states_k", g)][:, i, :].bitcast(F32).rearrange("p (row u) -> p row u", u=2)
            nc.scalar.copy(
                out=grouped,
                in_=turned[:].rearrange("p u row -> p row u"),
            )

        def quantise(g):
            if not exists(g):
                return
            words_q = work.tile([P, 2, GROUP_ROWS], U32, name="states_w", tag="states_w", align_bytes=64)
            scales_q = work.tile([P, 2, GROUP_ROWS], U8, name="states_s", tag="states_s", align_bytes=64)
            nc.vector.quantize_mx(
                out=words_q[:].rearrange("p s row -> p (s row)").bitcast(FP8X4),
                scales=scales_q[:].rearrange("p s row -> p (s row)"),
                in_=live[("states_k", g)][:].rearrange("p s k -> p (s k)"),
            )
            live[("main_q", g)] = (words_q[:, 0, :], scales_q[:, 0, :])
            live[("branch_q", g)] = (words_q[:, 1, :], scales_q[:, 1, :])

        def gate_sums(g, i):
            if not exists(g):
                return
            main_w, main_s = live[("main_q", g)]
            branch_w, branch_s = live[("branch_q", g)]
            sum_b = bank([P, STEP_CHUNKS, GROUP_ROWS])
            sum_mb = bank([P, STEP_CHUNKS, GROUP_ROWS])
            for a in range(STEP_CHUNKS):
                cols = slice((i * STEP_CHUNKS + a) * P, (i * STEP_CHUNKS + a + 1) * P)
                nc.tensor.matmul_mx(
                    out=sum_b[:, a, :], lhsT=w_words[:, 2, cols].bitcast(FP8X4), lhsT_scale=w_scales[:, 2, cols],
                    rhs=branch_w.bitcast(FP8X4), rhs_scale=branch_s, start=True, stop=True,
                )
            for a in range(STEP_CHUNKS):
                cols = slice((i * STEP_CHUNKS + a) * P, (i * STEP_CHUNKS + a + 1) * P)
                nc.tensor.matmul_mx(
                    out=sum_mb[:, a, :], lhsT=w_words[:, 0, cols].bitcast(FP8X4), lhsT_scale=w_scales[:, 0, cols],
                    rhs=main_w.bitcast(FP8X4), rhs_scale=main_s, start=True, stop=False,
                )
                nc.tensor.matmul_mx(
                    out=sum_mb[:, a, :], lhsT=w_words[:, 1, cols].bitcast(FP8X4), lhsT_scale=w_scales[:, 1, cols],
                    rhs=branch_w.bitcast(FP8X4), rhs_scale=branch_s, start=False, stop=True,
                )
            live[("sum_mb", g, i)] = sum_mb
            live[("sum_b", g, i)] = sum_b

        def gate_relu(g, i):
            if not exists(g):
                return
            weight_b = work.tile([P, STEP_CHUNKS, GROUP_ROWS], F32, name="weight_b", tag="weight_b")
            live[("weight_b", g, i)] = weight_b
            for a in range(STEP_CHUNKS):
                c = i * STEP_CHUNKS + a
                nc.scalar.activation(
                    out=weight_b[:, a, :], in_=live[("sum_mb", g, i)][:, a, :], func=ACT.Relu,
                    bias=bias_cols[:, c : c + 1], scale=1.0,
                )

        def gate_product(g, i):
            if not exists(g) or i < 0:
                return
            if i == 0:
                live[("h_m_t", g)] = work.tile([P, CHUNKS, GROUP_ROWS], F32, name="h_m_t", tag="h_m_t")
            for a in range(STEP_CHUNKS):
                c = i * STEP_CHUNKS + a
                nc.vector.scalar_tensor_tensor(
                    out=live[("h_m_t", g)][:, c, :], in0=live[("sum_b", g, i)][:, a, :],
                    scalar=bias_cols[:, CHUNKS + c : CHUNKS + c + 1], in1=live[("weight_b", g, i)][:, a, :],
                    op0=ALU.add, op1=ALU.mult,
                )

        def rows_back(g, t, use):
            if not exists(g):
                return
            h_m = bank([P, H])
            live[(use, g, t)] = h_m
            for c in range(CHUNKS):
                nc.tensor.transpose(
                    h_m[:, c * P : (c + 1) * P], live[("h_m_t", g)][:, c, t * P : (t + 1) * P], ident_f[:]
                )

        def square_main(g, t):
            if not exists(g):
                return
            nc.scalar.activation(
                out=unread()[:], in_=live[("main", g)][:, t, :], func=ACT.Square,
                accum_out=per_row("squares", g, 2 * TG)[:, t : t + 1],
            )

        def square_h_m(g, t):
            if not exists(g):
                return
            h_m = live[("to_square", g, t)]
            nc.scalar.activation(
                out=unread()[:], in_=h_m[:], func=ACT.Square,
                accum_out=per_row("squares", g, 2 * TG)[:, TG + t : TG + t + 1],
            )

        def lengths(g, t=None):
            if not exists(g):
                return
            some = slice(0, 2 * TG) if t is None else slice(t, 2 * TG, TG)
            count = 2 * TG if t is None else 2
            nc.gpsimd.tensor_tensor(
                out=per_row("lengths", g, 2 * TG)[:, some], in0=per_row("squares", g, 2 * TG)[:, some],
                in1=exp_half[:, 0:count], op=ALU.pow,
            )

        def alpha(g, part, t=None):
            if not exists(g):
                return
            lengths = per_row("lengths", g, 2 * TG)
            some = slice(0, TG) if t is None else slice(t, t + 1)
            if part == 0:
                nc.vector.scalar_tensor_tensor(
                    out=per_row("below", g)[:, some], in0=lengths[:, TG + some.start : TG + some.stop], scalar=BAG_EPS,
                    in1=lengths[:, some], op0=ALU.add, op1=ALU.max,
                )
            elif part == 1:
                nc.vector.reciprocal(out=per_row("inverse", g)[:, some], in_=per_row("below", g)[:, some])
            else:
                for a in range(some.start, some.stop):
                    nc.scalar.activation(
                        out=per_row("alpha", g)[:, a : a + 1], in_=per_row("inverse", g)[:, a : a + 1],
                        func=ACT.Copy, scale=lengths[:, a : a + 1],
                    )

        def shifted(g, t):
            if not exists(g):
                return
            h_m = live[("to_shift", g, t)]
            pre = work.tile([P, H], F32, name="pre", tag="pre", bufs=4)
            live[("pre", g, t)] = pre
            nc.vector.scalar_tensor_tensor(
                out=pre[:], in0=h_m[:], scalar=per_row("alpha", g)[:, t : t + 1],
                in1=live[("main", g)][:, t, :], op0=ALU.mult, op1=ALU.add,
                accum_out=per_row("total", g)[:, t : t + 1],
            )

        def mean(g, t=None):
            if not exists(g):
                return
            some = slice(0, TG) if t is None else slice(t, t + 1)
            nc.vector.tensor_scalar_mul(
                out=per_row("mean", g)[:, some], in0=per_row("total", g)[:, some], scalar1=1.0 / H
            )

        def variance(g, t):
            if not exists(g):
                return
            nc.scalar.activation(
                out=unread()[:], in_=live[("pre", g, t)][:], func=ACT.Square,
                bias=per_row("mean", g)[:, t : t + 1], scale=-1.0,
                accum_out=per_row("spread", g)[:, t : t + 1],
            )

        def centred(g, t):
            if not exists(g):
                return
            scaled = work.tile([P, H], F32, name="scaled", tag="scaled", bufs=4)
            live[("scaled", g, t)] = scaled
            nc.vector.scalar_tensor_tensor(
                out=scaled[:], in0=live[("pre", g, t)][:], scalar=per_row("mean", g)[:, t : t + 1],
                in1=ln_g_all[:], op0=ALU.subtract, op1=ALU.mult,
            )

        def bag_over_std(g, t=None):
            if not exists(g):
                return
            some = slice(0, TG) if t is None else slice(t, t + 1)
            tiles = slice(g * TG + some.start, g * TG + some.stop)
            nc.gpsimd.tensor_scalar(
                out=per_row("var", g)[:, some], in0=per_row("spread", g)[:, some], scalar1=1.0 / H, scalar2=LN_EPS,
                op0=ALU.mult, op1=ALU.add,
            )
            nc.gpsimd.tensor_tensor(
                out=per_row("rstd", g)[:, some], in0=per_row("var", g)[:, some], in1=exp_minus_half[:, some], op=ALU.pow
            )
            nc.gpsimd.tensor_tensor(
                out=per_row("bag_rstd", g)[:, some], in0=per_row("rstd", g)[:, some], in1=bag[:, tiles], op=ALU.mult
            )

        def carry_outer(g, t):
            if not exists(g):
                return
            live[("outer", g, t)] = bank([P, H])
            nc.tensor.matmul(
                out=live[("outer", g, t)][:], lhsT=bag_diag[:, g * TG + t, :], rhs=ln_b_all[:], start=True, stop=True
            )

        def carry(g, t):
            if not exists(g):
                return
            j = g * TG + t
            if t == 0:
                live[("shift_c", g)] = work.tile([P, 2, H], F32, name="shift_c", tag="shift_c", bufs=SHIFT_BUFS)
            nc.vector.scalar_tensor_tensor(
                out=live[("shift_c", g)][:, t, :], in0=live[("main", g)][:, t, :],
                scalar=not_bag[:, j : j + 1], in1=live[("outer", g, t)][:], op0=ALU.mult, op1=ALU.add,
            )

        def blend(g, t):
            if not exists(g):
                return
            shift_c = live[("shift_c", g)]
            nc.vector.scalar_tensor_tensor(
                out=shift_c[:, t, :], in0=live[("scaled", g, t)][:],
                scalar=per_row("bag_rstd", g)[:, t : t + 1], in1=shift_c[:, t, :],
                op0=ALU.mult, op1=ALU.add,
            )

        def store_shift(g, t=None):
            if not exists(g):
                return
            some = slice(0, TG) if t is None else slice(t, t + 1)
            tiles = slice(g * TG + some.start, g * TG + some.stop)
            nc.sync.dma_start(out=shift_v[:, tiles, :], in_=live[("shift_c", g)][:, some, :])

        def tanh(g, t=None):
            if not exists(g):
                return
            some = slice(0, TG) if t is None else slice(t, t + 1)
            if ("h", g) not in live:
                live[("h", g)] = work.tile([P, TG, H], F32, name="h", tag="h", bufs=8)
            nc.scalar.activation(out=live[("h", g)][:, some, :], in_=live[("shift_c", g)][:, some, :], func=ACT.Tanh)

        def gate_tanh(g, engine, t=None):
            if not exists(g):
                return
            h = live[("h", g)]
            some = slice(0, TG) if t is None else slice(t, t + 1)
            tiles = slice(g * TG + some.start, g * TG + some.stop)
            engine.tensor_tensor(
                out=h[:, some, :], in0=h[:, some, :], in1=live[("o", g)][:, some, :], op=ALU.mult
            )
            nc.sync.dma_start(out=h_v[:, tiles, :], in_=h[:, some, :])

        load_states(1)
        bag_diagonals(nc.vector, 0, 4)
        k_turn(0, 0)
        k_copy(0, 0)
        k_turn(0, 1)
        k_copy(0, 1)
        spread_ln_b()
        spread_biases()
        group_weights(0, 0)
        group_weights(0, 1)
        quantise(0)
        group_weights(1, 0)
        quantise_weights(0, 0)
        group_weights(2, 0)
        quantise_weights(1, 0)
        quantise_weights(2, 0)
        square_main(0, 0)
        square_main(0, 1)
        group_weights(1, 1)
        group_weights(2, 1)
        quantise_weights(0, 1)
        quantise_weights(1, 1)
        quantise_weights(2, 1)
        for g in range(2, 1 + AHEAD_STATES):
            load_states(g)
        for r in range(0, GROUPS - 1):
            load_states(r + 1 + AHEAD_STATES)
            load_o(r - 2 + AHEAD_O)
            if r == GROUPS - 2:
                load_o(GROUPS - 1)
            carry_outer(r, 0)
            carry(r, 0)
            alpha(r - 1, 1)
            gate_sums(r, 0)
            gate_relu(r, 0)
            k_turn(r + 1, 0)
            k_copy(r + 1, 0)
            gate_product(r, 0)
            alpha(r - 1, 2)
            carry_outer(r, 1)
            carry(r, 1)
            gate_sums(r, 1)
            gate_relu(r, 1)
            k_turn(r + 1, 1)
            k_copy(r + 1, 1)
            gate_product(r, 1)
            rows_back(r - 1, 0, "to_shift")
            shifted(r - 1, 0)
            square_main(r + 1, 0)
            rows_back(r - 1, 1, "to_shift")
            shifted(r - 1, 1)
            quantise(r + 1)
            mean(r - 1)
            if r == 0:
                spread_ln_g()
                bag_diagonals(nc.vector, 4, TILES)
            rows_back(r, 0, "to_square")
            square_h_m(r, 0)
            rows_back(r, 1, "to_square")
            square_h_m(r, 1)
            square_main(r + 1, 1)
            lengths(r)
            blend(r - 2, 0)
            blend(r - 2, 1)
            store_shift(r - 2)
            variance(r - 1, 0)
            centred(r - 1, 0)
            variance(r - 1, 1)
            centred(r - 1, 1)
            alpha(r, 0)
            bag_over_std(r - 1)
            tanh(r - 2)
            gate_tanh(r - 2, nc.gpsimd)
        last = GROUPS - 1
        carry_outer(last, 0)
        carry_outer(last, 1)
        gate_sums(last, 0)
        gate_relu(last, 0)
        alpha(last - 1, 1)
        carry(last, 0)
        gate_product(last, 0)
        gate_sums(last, 1)
        gate_relu(last, 1)
        alpha(last - 1, 2)
        gate_product(last, 1)
        rows_back(last - 1, 0, "to_shift")
        rows_back(last - 1, 1, "to_shift")
        rows_back(last, 0, "to_square")
        rows_back(last, 1, "to_square")
        shifted(last - 1, 0)
        shifted(last - 1, 1)
        square_h_m(last, 0)
        lengths(last, 0)
        square_h_m(last, 1)
        lengths(last, 1)
        carry(last, 1)
        mean(last - 1)
        variance(last - 1, 0)
        variance(last - 1, 1)
        alpha(last, 0, 0)
        blend(last - 2, 0)
        alpha(last, 1, 0)
        blend(last - 2, 1)
        store_shift(last - 2)
        alpha(last, 2, 0)
        alpha(last, 0, 1)
        bag_over_std(last - 1)
        rows_back(last, 0, "to_shift")
        rows_back(last, 1, "to_shift")
        shifted(last, 0)
        alpha(last, 1, 1)
        mean(last, 0)
        alpha(last, 2, 1)
        shifted(last, 1)
        variance(last, 0)
        bag_over_std(last, 0)
        centred(last - 1, 0)
        mean(last, 1)
        variance(last, 1)
        bag_over_std(last, 1)
        tanh(last - 2)
        centred(last - 1, 1)
        blend(last - 1, 0)
        blend(last - 1, 1)
        store_shift(last - 1)
        tanh(last - 1)
        centred(last, 0)
        centred(last, 1)
        blend(last, 0)
        store_shift(last, 0)
        tanh(last, 0)
        gate_tanh(last - 2, nc.vector)
        blend(last, 1)
        store_shift(last, 1)
        tanh(last, 1)
        gate_tanh(last - 1, nc.vector)
        gate_tanh(last, nc.vector, 0)
        gate_tanh(last, nc.vector, 1)
